import numpy as np
import ml_dtypes


def mxq(x, axis, fmt="e4m3"):
    dtype, down = {"e4m3": (ml_dtypes.float8_e4m3fn, 7), "e5m2": (ml_dtypes.float8_e5m2, 14)}[fmt]
    v = np.moveaxis(np.asarray(x, np.float32).astype(ml_dtypes.bfloat16).astype(np.float64), axis, -1)
    blocks = v.reshape(v.shape[:-1] + (-1, 32))
    amax = np.abs(blocks).max(-1, keepdims=True)
    byte = np.maximum(np.where(amax > 0, np.frexp(amax)[1] - 1 + 127, 0) - down, 1)
    scale = np.exp2(byte - 127.0)
    codes = (blocks / scale).astype(np.float32).astype(dtype).astype(np.float64)
    return np.moveaxis((codes * scale).reshape(v.shape), -1, axis)


WIDE = False


def mx_kscale(k):
    if not WIDE:
        return np.ones(k)
    levels = np.array([10, -10, 5, -5, 0])
    a = np.random.permutation(np.resize(levels, k // 512 * 4)).reshape(k // 512, 4)
    idx = np.arange(k)
    return np.exp2(a[idx // 512, idx % 128 // 32])


BF16 = ml_dtypes.bfloat16


def bf(x):
    return np.asarray(x, np.float32).astype(BF16)


def f64(x):
    return np.asarray(x).astype(np.float64)


B, P, D, NL, T, E, G = 8, 512, 512, 8, 2, 1, 2
WG = NL * NL * T * G
CLIP = 1.0
LOG_2PI = np.log(2.0 * np.pi)


def clip(v):
    return np.clip(v, -CLIP, CLIP)


def gaussian_multi(m1, v1, m2, v2):
    v1s = np.exp(2.0 * v1)
    v2s = np.exp(2.0 * v2)
    add = v1s + v2s
    log_add = np.log(add)
    scale = (-0.5 * (LOG_2PI + log_add + (m1 - m2) ** 2 / add)).sum(-1)
    mu = (m1 * v2s + m2 * v1s) / add
    var = v1 + v2 - 0.5 * log_add
    return scale, mu, var


def setup_inputs():
    s = mx_kscale(D)
    return {"x": bf(np.random.standard_normal((B, P, D)) * s),
            "s_weight": bf(np.random.standard_normal((B, P, NL, E))),
            "s_mu": bf(clip(np.random.standard_normal((B, P, NL, E, G)))),
            "s_var": bf(clip(np.random.standard_normal((B, P, NL, E, G)))),
            "tcm_w": bf(np.random.standard_normal((D, WG)) / np.sqrt(D) / s[:, None]),
            "tcm_b": bf(np.random.standard_normal(WG) * 0.3),
            "tcv_w": bf(np.random.standard_normal((D, WG)) / np.sqrt(D) / s[:, None]),
            "tcv_b": bf(np.random.standard_normal(WG) * 0.3)}


def reference(x, s_weight, s_mu, s_var, tcm_w, tcm_b, tcv_w, tcv_b):
    xq = mxq(f64(x).reshape(B * P, D), 1, "e4m3")
    t_c_mu = clip(((xq @ mxq(f64(tcm_w), 0, "e4m3")) + f64(tcm_b)).reshape(B, P, NL, NL, T, G))[:, :, :, :, :, None, :]
    t_c_var = clip(((xq @ mxq(f64(tcv_w), 0, "e4m3")) + f64(tcv_b)).reshape(B, P, NL, NL, T, G))[:, :, :, :, :, None, :]
    m1 = f64(s_mu)[:, :, None, :, None, :, :]
    v1 = f64(s_var)[:, :, None, :, None, :, :]
    cs_scale, cs_mu, cs_var = gaussian_multi(m1, v1, t_c_mu, t_c_var)
    cs_scale = cs_scale + f64(s_weight)[:, :, None, :, None, :]
    return cs_scale, cs_mu, cs_var

@@ -1,0 +1,338 @@
+import math
+from contextlib import ExitStack
+
+import concourse.masks as masks
+import concourse.mybir as mybir
+
+F32 = mybir.dt.float32
+BF16 = mybir.dt.bfloat16
+U32 = mybir.dt.uint32
+U8 = mybir.dt.uint8
+FP8X4 = mybir.dt.float8_e4m3fn_x4
+ALU = mybir.AluOpType
+ACT = mybir.ActivationFunctionType
+
+FLOPS = 2 * 4096 * 512 * 512
+
+P = 128
+NT = 32
+ST = 4
+K = 512
+NC = 256
+GROUPS = ((0,), (1,), (2, 3), (4, 5), (6, 7))
+POOL_DA = False
+POOL_P1 = False
+
+
+def tile_chainlveg_pa_t_kernel(
+    tc, x, s_weight, s_mu, s_var, tcm_w, tcm_b, tcv_w, tcv_b, out_0, out_1, out_2
+):
+    nc = tc.nc
+    xv = x.rearrange("b (c n) k -> (b c) n k", n=NT)
+    sc_v = out_0.rearrange("b (c n) i j t e -> (b c) n (i j t e)", n=NT)
+    mu_v = out_1.rearrange("b (c n) i j t e g -> (b c) n (i j t e g)", n=NT)
+    var_v = out_2.rearrange("b (c n) i j t e g -> (b c) n (i j t e g)", n=NT)
+    smu_v = s_mu.rearrange("b (c n) j e g -> (b c) (n j e g)", n=NT)
+    svar_v = s_var.rearrange("b (c n) j e g -> (b c) (n j e g)", n=NT)
+    sw_v = s_weight.rearrange("b (c n) j e -> (b c) (n j e)", n=NT)
+
+    with ExitStack() as ctx:
+        const = ctx.enter_context(tc.tile_pool(name="const", bufs=1))
+        grp_pool = ctx.enter_context(tc.tile_pool(name="grp", bufs=2))
+        xq_pool = ctx.enter_context(tc.tile_pool(name="xq", bufs=4))
+        y1m_pool = ctx.enter_context(tc.tile_pool(name="y1m", bufs=3))
+        y1v_pool = ctx.enter_context(tc.tile_pool(name="y1v", bufs=2))
+        y2v_pool = ctx.enter_context(tc.tile_pool(name="y2v", bufs=6))
+        out_pool = ctx.enter_context(tc.tile_pool(name="outp", bufs=3))
+        sum_pool = ctx.enter_context(tc.tile_pool(name="sump", bufs=2))
+        psum = ctx.enter_context(tc.psum_pool(name="psum", bufs=2))
+        ctx.enter_context(tc.manual_schedule())
+
+        x_sb = const.tile([P, NT, K], BF16, name="x_sb")
+        wraw = const.tile([P, 4, 2 * NC], BF16, name="wraw")
+        bz = const.tile([P, P], BF16, name="bz")
+        smu = const.tile([P, NT * 16], BF16, name="smu")
+        svar = const.tile([P, NT * 16], BF16, name="svar")
+        sw = const.tile([P, NT * 8], BF16, name="sw")
+        nc.vector.memset(bz[:], 0.0)
+        nc.sync.dma_start(out=x_sb[:, 0:ST, :], in_=xv[:, 0:ST, :])
+        for u in range(2):
+            for w, off in ((tcm_w, 0), (tcv_w, NC)):
+                nc.sync.dma_start(
+                    out=wraw[:, 2 * u : 2 * u + 2, off : off + NC],
+                    in_=w[256 * u : 256 * u + 256, :].rearrange("(q e) c -> q e c", e=2),
+                )
+        nc.sync.dma_start(out=bz[0:2, :], in_=tcm_b.rearrange("(r c) -> r c", r=2))
+        nc.sync.dma_start(out=bz[2:4, :], in_=tcv_b.rearrange("(r c) -> r c", r=2))
+        nc.sync.dma_start(out=x_sb[:, ST : 2 * ST, :], in_=xv[:, ST : 2 * ST, :])
+        nc.sync.dma_start(out=svar[:], in_=svar_v)
+        nc.sync.dma_start(out=smu[:], in_=smu_v)
+        nc.sync.dma_start(out=sw[:], in_=sw_v)
+        for s in range(2, NT // ST):
+            nc.sync.dma_start(
+                out=x_sb[:, s * ST : (s + 1) * ST, :], in_=xv[:, s * ST : (s + 1) * ST, :]
+            )
+
+        ident = const.tile([P, P], F32, name="ident")
+        masks.make_identity(nc, ident[:])
+        two = const.tile([P, 1], F32, name="two")
+        nc.vector.memset(two[:], 2.0)
+
+        wgrp = const.tile([P, 2 * NC, 4], BF16, name="wgrp", align_bytes=64)
+        wq = const.tile([P, 2 * NC], U32, name="wq", align_bytes=64)
+        wsc = const.tile([P, 2 * NC], U8, name="wsc", align_bytes=64)
+        nc.vector.tensor_copy(out=wgrp[:], in_=wraw[:].rearrange("p t c -> p c t"))
+        bf = const.tile([P, P], F32, name="bf")
+        nc.vector.tensor_copy(out=bf[:], in_=bz[:])
+        nc.vector.quantize_mx(
+            out=wq[:].bitcast(FP8X4), scales=wsc[:], in_=wgrp[:].rearrange("p c t -> p (c t)")
+        )
+        bt = psum.tile([P, 512], F32, name="bt", tag="xt")
+        nc.tensor.transpose(bt[:, 0:P], bf[:], ident[:])
+        b1 = const.tile([P, 4], F32, name="b1")
+        nc.vector.tensor_scalar_add(out=b1[:], in0=bt[:, 0:4], scalar1=1.0)
+
+        dnu = const.tile([P, NT, 2 * NC], F32, name="dnu")
+        m1e = const.tile([P, NT, 32], F32, name="m1e")
+        m1p = const.tile([P, NT, 32], F32, name="m1p")
+        v1p = const.tile([P, NT, 32], F32, name="v1p")
+        hae = const.tile([P, NT, 32], F32, name="hae")
+        vs = const.tile([P, NT * 8], F32, name="vs")
+        k0 = const.tile([P, NT * 8], F32, name="k0")
+        ke = const.tile([P, NT, 16], F32, name="ke")
+
+        live = {}
+
+        def spread(small):
+            return (
+                small[:]
+                .rearrange("p (a g) -> p a g", g=2)
+                .unsqueeze(2)
+                .to_broadcast([P, NT * 8, 2, 2])
+            )
+
+        def as_njtg(full):
+            return full[:].rearrange("p n (j t g) -> p (n j) t g", t=2, g=2)
+
+        def prepare_state():
+            nc.scalar.activation(out=as_njtg(hae), in_=spread(svar), func=ACT.Exp, scale=-2.0)
+            nc.vector.tensor_scalar(
+                out=as_njtg(v1p), in0=spread(svar), scalar1=-1.0, scalar2=1.0,
+                op0=ALU.mult, op1=ALU.add,
+            )
+            nc.vector.tensor_copy(out=as_njtg(m1e), in_=spread(smu))
+            nc.vector.tensor_scalar_add(out=m1p[:], in0=m1e[:], scalar1=1.0)
+            nc.vector.tensor_scalar_mul(out=hae[:], in0=hae[:], scalar1=0.5)
+            pairs = svar[:].rearrange("p (a g) -> p a g", g=2)
+            nc.vector.tensor_tensor(out=vs[:], in0=pairs[:, :, 0], in1=pairs[:, :, 1], op=ALU.add)
+            nc.vector.scalar_tensor_tensor(
+                out=k0[:], in0=sw[:], scalar=-(math.log(2.0 * math.pi) + 2.0), in1=vs[:],
+                op0=ALU.add, op1=ALU.subtract,
+            )
+            nc.vector.tensor_copy(
+                out=ke[:].rearrange("p n (j t) -> p (n j) t", t=2),
+                in_=k0[:].unsqueeze(2).to_broadcast([P, NT * 8, 2]),
+            )
+
+        def x_transpose(s, h):
+            if h == 0:
+                live[("grp", s)] = grp_pool.tile([P, 4 * 512], BF16, name="grp", align_bytes=64)
+            grp = live[("grp", s)]
+            xt = psum.tile([P, 2, 256], F32, name="xt", tag="xt")
+            for j in range(2):
+                words = x_sb[:, s * ST + 2 * h + j, :].bitcast(F32)
+                for u in range(2):
+                    nc.tensor.transpose(
+                        xt[:, u, j * P : (j + 1) * P], words[:, u * P : (u + 1) * P], ident[:]
+                    )
+            nc.scalar.copy(
+                out=grp[:].bitcast(F32)[:, h * 512 : (h + 1) * 512].rearrange(
+                    "p (r u) -> p r u", u=2
+                ),
+                in_=xt[:].rearrange("p u r -> p r u"),
+            )
+
+        def x_quantise(s):
+            xq = xq_pool.tile([P, 512], U32, name="xq", align_bytes=64)
+            xs = xq_pool.tile([P, 512], U8, name="xs", align_bytes=64)
+            live[("xq", s)] = (xq, xs)
+            nc.vector.quantize_mx(
+                out=xq[:].bitcast(FP8X4), scales=xs[:], in_=live[("grp", s)][:]
+            )
+
+        def project(s, cb):
+            xq, xs = live[("xq", s)]
+            if cb == 2:
+                live[("y1v", s)] = y1v_pool.tile([P, 2, 512], F32, name="y1v")
+            if cb == 0:
+                live[("y1m", s)] = y1m_pool.tile([P, 2, 512], F32, name="y1m")
+            pc = psum.tile([P, 512], F32, name="pc", tag="pc")
+            nc.tensor.matmul_mx(
+                out=pc[:],
+                lhsT=wq[:, cb * P : (cb + 1) * P].bitcast(FP8X4),
+                lhsT_scale=wsc[:, cb * P : (cb + 1) * P],
+                rhs=xq[:].bitcast(FP8X4),
+                rhs_scale=xs[:],
+                start=True,
+                stop=True,
+            )
+            dest = live[("y1m", s)][:, cb, :] if cb < 2 else live[("y1v", s)][:, cb - 2, :]
+            nc.scalar.activation(
+                out=dest, in_=pc[:], func=ACT.Relu, bias=b1[:, cb : cb + 1], scale=1.0
+            )
+            if cb == 3:
+                y2v = y2v_pool.tile([P, 2, 512], F32, name="y2v")
+                live[("y2v", s)] = y2v
+                nc.scalar.activation(
+                    out=y2v[:], in_=live[("y1v", s)][:], func=ACT.Relu, bias=two[:], scale=-1.0
+                )
+
+        def back_transpose(s, tl):
+            n = s * ST + tl
+            y1m = live[("y1m", s)]
+            y2v = live[("y2v", s)]
+            yt = psum.tile([P, 512], F32, name="yt", tag="yt")
+            for cb in range(2):
+                nc.tensor.transpose(
+                    yt[:, cb * P : (cb + 1) * P], y1m[:, cb, tl * P : (tl + 1) * P], ident[:]
+                )
+            for cb in range(2):
+                nc.tensor.transpose(
+                    yt[:, NC + cb * P : NC + (cb + 1) * P],
+                    y2v[:, cb, tl * P : (tl + 1) * P],
+                    ident[:],
+                )
+            nc.vector.scalar_tensor_tensor(
+                out=dnu[:, n, 0:NC].rearrange("p (i c) -> p i c", i=8),
+                in0=yt[:, 0:NC].rearrange("p (i c) -> p i c", i=8),
+                scalar=2.0,
+                in1=m1p[:, n, :].unsqueeze(1).to_broadcast([P, 8, 32]),
+                op0=ALU.min,
+                op1=ALU.subtract,
+            )
+            nc.vector.tensor_tensor(
+                out=dnu[:, n, NC : 2 * NC].rearrange("p (i c) -> p i c", i=8),
+                in0=yt[:, NC : 2 * NC].rearrange("p (i c) -> p i c", i=8),
+                in1=v1p[:, n, :].unsqueeze(1).to_broadcast([P, 8, 32]),
+                op=ALU.subtract,
+            )
+
+        def rows(s):
+            return slice(s * ST, (s + 1) * ST)
+
+        def over_i(small, s, width):
+            return small[:, rows(s), :].unsqueeze(2).to_broadcast([P, ST, 8, width])
+
+        def split_i(ap):
+            return ap.rearrange("p n (i c) -> p n i c", i=8)
+
+        def scaled_diff(s):
+            eng = nc.gpsimd if POOL_DA else nc.vector
+            dn = split_i(dnu[:, rows(s), 0:NC])
+            eng.tensor_tensor(out=dn, in0=dn, in1=over_i(hae, s, 32), op=ALU.mult)
+
+        def sigmoid(s):
+            nu = dnu[:, rows(s), NC : 2 * NC]
+            nc.scalar.activation(out=nu, in_=nu, func=ACT.Sigmoid, scale=2.0)
+
+        def gain(s):
+            g = out_pool.tile([P, ST, NC], F32, name="gmu")
+            live[("g", s)] = g
+            nc.vector.tensor_tensor(
+                out=g[:], in0=dnu[:, rows(s), 0:NC], in1=dnu[:, rows(s), NC : 2 * NC], op=ALU.mult
+            )
+
+        def mean(s):
+            g = live[("g", s)]
+            dn = dnu[:, rows(s), 0:NC]
+            scaled_diff(s)
+            nc.vector.tensor_tensor(out=dn, in0=g[:], in1=dn, op=ALU.mult)
+            nc.vector.tensor_tensor(
+                out=split_i(g[:]), in0=split_i(g[:]), in1=over_i(m1e, s, 32), op=ALU.add
+            )
+            nc.sync.dma_start(out=mu_v[:, rows(s), :], in_=g[:])
+
+        def log_weight(s):
+            wc = dnu[:, rows(s), NC : 2 * NC]
+            nc.scalar.activation(out=wc, in_=wc, func=ACT.Ln, scale=math.exp(2.0))
+
+        def half_terms(s):
+            nc.vector.scalar_tensor_tensor(
+                out=dnu[:, rows(s), 0:NC],
+                in0=dnu[:, rows(s), NC : 2 * NC],
+                scalar=0.5,
+                in1=dnu[:, rows(s), 0:NC],
+                op0=ALU.mult,
+                op1=ALU.subtract,
+            )
+
+        def variance(s, h):
+            if h == 0:
+                live[("var", s)] = out_pool.tile([P, ST, NC], F32, name="var")
+            vt = live[("var", s)]
+            y2v = live[("y2v", s)]
+            yv = psum.tile([P, 2, NC], F32, name="yv", tag="yv")
+            for j in range(2):
+                tl = 2 * h + j
+                for cb in range(2):
+                    nc.tensor.transpose(
+                        yv[:, j, cb * P : (cb + 1) * P], y2v[:, cb, tl * P : (tl + 1) * P], ident[:]
+                    )
+            n = s * ST + 2 * h
+            nc.vector.scalar_tensor_tensor(
+                out=vt[:, 2 * h : 2 * h + 2, :],
+                in0=dnu[:, n : n + 2, NC : 2 * NC],
+                scalar=0.5,
+                in1=yv[:],
+                op0=ALU.mult,
+                op1=ALU.subtract,
+            )
+            if h == 1:
+                nc.sync.dma_start(out=var_v[:, rows(s), :], in_=vt[:])
+
+        def log_scale(s):
+            eng = nc.gpsimd if POOL_P1 else nc.vector
+            pair = dnu[:, rows(s), 0:NC].rearrange("p n (c g) -> p n c g", g=2)
+            ps = sum_pool.tile([P, ST, P], F32, name="ps")
+            eng.tensor_tensor(out=ps[:], in0=pair[:, :, :, 0], in1=pair[:, :, :, 1], op=ALU.add)
+            sc = out_pool.tile([P, ST, P], F32, name="sc")
+            nc.vector.tensor_tensor(
+                out=split_i(sc[:]), in0=split_i(ps[:]), in1=over_i(ke, s, 16), op=ALU.add
+            )
+            nc.sync.dma_start(out=sc_v[:, rows(s), :], in_=sc[:])
+
+        def members(gi):
+            return GROUPS[gi] if 0 <= gi < len(GROUPS) else ()
+
+        def weave(first, second):
+            for i in range(max(len(first), len(second))):
+                if i < len(first):
+                    first[i][0](*first[i][1])
+                if i < len(second):
+                    second[i][0](*second[i][1])
+
+        for step in range(-2, len(GROUPS) + 1):
+            weave(
+                [(back_transpose, (s, tl)) for s in members(step) for tl in range(ST)],
+                [(project, (s, cb)) for s in members(step + 1) for cb in (2, 3, 0, 1)],
+            )
+            for s in members(step - 1):
+                half_terms(s)
+            weave(
+                [(x_transpose, (s, h)) for s in members(step + 2) for h in range(2)],
+                [(variance, (s, h)) for s in members(step - 1) for h in range(2)],
+            )
+            for s in members(step - 1):
+                log_scale(s)
+            for s in members(step + 2):
+                x_quantise(s)
+            if step == -2:
+                prepare_state()
+            for s in members(step):
+                sigmoid(s)
+            for s in members(step):
+                gain(s)
+            for s in members(step):
+                mean(s)
+            for s in members(step):
+                log_weight(s)

@@ -19,9 +19,12 @@ NT = 32
 ST = 4
 K = 512
 NC = 256
-GROUPS = ((0,), (1,), (2, 3), (4, 5), (6, 7))
-POOL_DA = False
+GROUPS = ((0,), (1,), (2,), (3,), (4,), (5,), (6,), (7,))
+POOL_DA = True
 POOL_P1 = False
+POOL_P2 = False
+RING = {"grp": 2, "xq": 2, "y1m": 2, "y1v": 2, "y2v": 4, "da": 3, "out": 3, "sum": 2}
+PLAN = (("q", 2), ("ln", -1), ("xt", 3), ("bt", 1), ("va", -1), ("mm", 2), ("ms", 0), ("sg", 1), ("es", -1), ("p2", -1))
 
 
 def tile_chainlveg_pa_t_kernel(
@@ -38,14 +41,15 @@ def tile_chainlveg_pa_t_kernel(
 
     with ExitStack() as ctx:
         const = ctx.enter_context(tc.tile_pool(name="const", bufs=1))
-        grp_pool = ctx.enter_context(tc.tile_pool(name="grp", bufs=2))
-        xq_pool = ctx.enter_context(tc.tile_pool(name="xq", bufs=4))
-        y1m_pool = ctx.enter_context(tc.tile_pool(name="y1m", bufs=3))
-        y1v_pool = ctx.enter_context(tc.tile_pool(name="y1v", bufs=2))
-        y2v_pool = ctx.enter_context(tc.tile_pool(name="y2v", bufs=6))
-        out_pool = ctx.enter_context(tc.tile_pool(name="outp", bufs=3))
-        sum_pool = ctx.enter_context(tc.tile_pool(name="sump", bufs=2))
-        psum = ctx.enter_context(tc.psum_pool(name="psum", bufs=2))
+        grp_pool = ctx.enter_context(tc.tile_pool(name="grp", bufs=RING["grp"]))
+        xq_pool = ctx.enter_context(tc.tile_pool(name="xq", bufs=RING["xq"]))
+        y1m_pool = ctx.enter_context(tc.tile_pool(name="y1m", bufs=RING["y1m"]))
+        da_pool = ctx.enter_context(tc.tile_pool(name="da", bufs=RING["da"]))
+        y1v_pool = ctx.enter_context(tc.tile_pool(name="y1v", bufs=RING["y1v"]))
+        y2v_pool = ctx.enter_context(tc.tile_pool(name="y2v", bufs=RING["y2v"]))
+        out_pool = ctx.enter_context(tc.tile_pool(name="outp", bufs=RING["out"]))
+        sum_pool = ctx.enter_context(tc.tile_pool(name="sump", bufs=RING["sum"]))
+        psum = ctx.enter_context(tc.psum_pool(name="psum", bufs=4))
         ctx.enter_context(tc.manual_schedule())
 
         x_sb = const.tile([P, NT, K], BF16, name="x_sb")
@@ -55,19 +59,19 @@ def tile_chainlveg_pa_t_kernel(
         svar = const.tile([P, NT * 16], BF16, name="svar")
         sw = const.tile([P, NT * 8], BF16, name="sw")
         nc.vector.memset(bz[:], 0.0)
+        nc.scalar.dma_start(out=svar[:], in_=svar_v)
         nc.sync.dma_start(out=x_sb[:, 0:ST, :], in_=xv[:, 0:ST, :])
+        nc.scalar.dma_start(out=smu[:], in_=smu_v)
+        nc.scalar.dma_start(out=sw[:], in_=sw_v)
+        nc.scalar.dma_start(out=bz[0:2, :], in_=tcm_b.rearrange("(r c) -> r c", r=2))
+        nc.scalar.dma_start(out=bz[2:4, :], in_=tcv_b.rearrange("(r c) -> r c", r=2))
         for u in range(2):
             for w, off in ((tcm_w, 0), (tcv_w, NC)):
                 nc.sync.dma_start(
                     out=wraw[:, 2 * u : 2 * u + 2, off : off + NC],
                     in_=w[256 * u : 256 * u + 256, :].rearrange("(q e) c -> q e c", e=2),
                 )
-        nc.sync.dma_start(out=bz[0:2, :], in_=tcm_b.rearrange("(r c) -> r c", r=2))
-        nc.sync.dma_start(out=bz[2:4, :], in_=tcv_b.rearrange("(r c) -> r c", r=2))
         nc.sync.dma_start(out=x_sb[:, ST : 2 * ST, :], in_=xv[:, ST : 2 * ST, :])
-        nc.sync.dma_start(out=svar[:], in_=svar_v)
-        nc.sync.dma_start(out=smu[:], in_=smu_v)
-        nc.sync.dma_start(out=sw[:], in_=sw_v)
         for s in range(2, NT // ST):
             nc.sync.dma_start(
                 out=x_sb[:, s * ST : (s + 1) * ST, :], in_=xv[:, s * ST : (s + 1) * ST, :]
@@ -81,16 +85,20 @@ def tile_chainlveg_pa_t_kernel(
         wgrp = const.tile([P, 2 * NC, 4], BF16, name="wgrp", align_bytes=64)
         wq = const.tile([P, 2 * NC], U32, name="wq", align_bytes=64)
         wsc = const.tile([P, 2 * NC], U8, name="wsc", align_bytes=64)
-        nc.vector.tensor_copy(out=wgrp[:], in_=wraw[:].rearrange("p t c -> p c t"))
         bf = const.tile([P, P], F32, name="bf")
-        nc.vector.tensor_copy(out=bf[:], in_=bz[:])
-        nc.vector.quantize_mx(
-            out=wq[:].bitcast(FP8X4), scales=wsc[:], in_=wgrp[:].rearrange("p c t -> p (c t)")
-        )
-        bt = psum.tile([P, 512], F32, name="bt", tag="xt")
-        nc.tensor.transpose(bt[:, 0:P], bf[:], ident[:])
         b1 = const.tile([P, 4], F32, name="b1")
-        nc.vector.tensor_scalar_add(out=b1[:], in0=bt[:, 0:4], scalar1=1.0)
+
+        def prepare_weights():
+            nc.vector.tensor_copy(out=wgrp[:], in_=wraw[:].rearrange("p t c -> p c t"))
+            nc.vector.tensor_copy(out=bf[:], in_=bz[:])
+            nc.vector.quantize_mx(
+                out=wq[:].bitcast(FP8X4), scales=wsc[:], in_=wgrp[:].rearrange("p c t -> p (c t)")
+            )
+
+        def bias_columns():
+            bt = psum.tile([P, 512], F32, name="bt", tag="pa")
+            nc.tensor.transpose(bt[:, 0:P], bf[:], ident[:])
+            nc.vector.tensor_scalar_add(out=b1[:], in0=bt[:, 0:4], scalar1=1.0)
 
         dnu = const.tile([P, NT, 2 * NC], F32, name="dnu")
         m1e = const.tile([P, NT, 32], F32, name="m1e")
@@ -115,13 +123,15 @@ def tile_chainlveg_pa_t_kernel(
             return full[:].rearrange("p n (j t g) -> p (n j) t g", t=2, g=2)
 
         def prepare_state():
-            nc.scalar.activation(out=as_njtg(hae), in_=spread(svar), func=ACT.Exp, scale=-2.0)
             nc.vector.tensor_scalar(
                 out=as_njtg(v1p), in0=spread(svar), scalar1=-1.0, scalar2=1.0,
                 op0=ALU.mult, op1=ALU.add,
             )
             nc.vector.tensor_copy(out=as_njtg(m1e), in_=spread(smu))
             nc.vector.tensor_scalar_add(out=m1p[:], in0=m1e[:], scalar1=1.0)
+
+        def prepare_rest():
+            nc.scalar.activation(out=as_njtg(hae), in_=spread(svar), func=ACT.Exp, scale=-2.0)
             nc.vector.tensor_scalar_mul(out=hae[:], in0=hae[:], scalar1=0.5)
             pairs = svar[:].rearrange("p (a g) -> p a g", g=2)
             nc.vector.tensor_tensor(out=vs[:], in0=pairs[:, :, 0], in1=pairs[:, :, 1], op=ALU.add)
@@ -138,7 +148,7 @@ def tile_chainlveg_pa_t_kernel(
             if h == 0:
                 live[("grp", s)] = grp_pool.tile([P, 4 * 512], BF16, name="grp", align_bytes=64)
             grp = live[("grp", s)]
-            xt = psum.tile([P, 2, 256], F32, name="xt", tag="xt")
+            xt = psum.tile([P, 2, 256], F32, name="xt", tag="pa")
             for j in range(2):
                 words = x_sb[:, s * ST + 2 * h + j, :].bitcast(F32)
                 for u in range(2):
@@ -166,7 +176,7 @@ def tile_chainlveg_pa_t_kernel(
                 live[("y1v", s)] = y1v_pool.tile([P, 2, 512], F32, name="y1v")
             if cb == 0:
                 live[("y1m", s)] = y1m_pool.tile([P, 2, 512], F32, name="y1m")
-            pc = psum.tile([P, 512], F32, name="pc", tag="pc")
+            pc = psum.tile([P, 512], F32, name="pc", tag="pa")
             nc.tensor.matmul_mx(
                 out=pc[:],
                 lhsT=wq[:, cb * P : (cb + 1) * P].bitcast(FP8X4),
@@ -191,7 +201,7 @@ def tile_chainlveg_pa_t_kernel(
             n = s * ST + tl
             y1m = live[("y1m", s)]
             y2v = live[("y2v", s)]
-            yt = psum.tile([P, 512], F32, name="yt", tag="yt")
+            yt = psum.tile([P, 512], F32, name="yt", tag="pv")
             for cb in range(2):
                 nc.tensor.transpose(
                     yt[:, cb * P : (cb + 1) * P], y1m[:, cb, tl * P : (tl + 1) * P], ident[:]
@@ -227,9 +237,23 @@ def tile_chainlveg_pa_t_kernel(
             return ap.rearrange("p n (i c) -> p n i c", i=8)
 
         def scaled_diff(s):
-            eng = nc.gpsimd if POOL_DA else nc.vector
-            dn = split_i(dnu[:, rows(s), 0:NC])
-            eng.tensor_tensor(out=dn, in0=dn, in1=over_i(hae, s, 32), op=ALU.mult)
+            da = da_pool.tile([P, ST, NC], F32, name="da")
+            live[("da", s)] = da
+            nc.vector.tensor_tensor(
+                out=split_i(da[:]), in0=split_i(dnu[:, rows(s), 0:NC]), in1=over_i(hae, s, 32),
+                op=ALU.mult,
+            )
+
+        def scaled_diff_tile(s, tl):
+            if tl == 0:
+                live[("da", s)] = da_pool.tile([P, ST, NC], F32, name="da")
+            n = s * ST + tl
+            nc.gpsimd.tensor_tensor(
+                out=live[("da", s)][:, tl, :].rearrange("p (i c) -> p i c", i=8),
+                in0=dnu[:, n, 0:NC].rearrange("p (i c) -> p i c", i=8),
+                in1=hae[:, n, :].unsqueeze(1).to_broadcast([P, 8, 32]),
+                op=ALU.mult,
+            )
 
         def sigmoid(s):
             nu = dnu[:, rows(s), NC : 2 * NC]
@@ -245,8 +269,9 @@ def tile_chainlveg_pa_t_kernel(
         def mean(s):
             g = live[("g", s)]
             dn = dnu[:, rows(s), 0:NC]
-            scaled_diff(s)
-            nc.vector.tensor_tensor(out=dn, in0=g[:], in1=dn, op=ALU.mult)
+            if not POOL_DA:
+                scaled_diff(s)
+            nc.vector.tensor_tensor(out=dn, in0=g[:], in1=live[("da", s)][:], op=ALU.mult)
             nc.vector.tensor_tensor(
                 out=split_i(g[:]), in0=split_i(g[:]), in1=over_i(m1e, s, 32), op=ALU.add
             )
@@ -271,7 +296,7 @@ def tile_chainlveg_pa_t_kernel(
                 live[("var", s)] = out_pool.tile([P, ST, NC], F32, name="var")
             vt = live[("var", s)]
             y2v = live[("y2v", s)]
-            yv = psum.tile([P, 2, NC], F32, name="yv", tag="yv")
+            yv = psum.tile([P, 2, NC], F32, name="yv", tag="pv")
             for j in range(2):
                 tl = 2 * h + j
                 for cb in range(2):
@@ -290,13 +315,18 @@ def tile_chainlveg_pa_t_kernel(
             if h == 1:
                 nc.sync.dma_start(out=var_v[:, rows(s), :], in_=vt[:])
 
-        def log_scale(s):
+        def pair_sum(s):
             eng = nc.gpsimd if POOL_P1 else nc.vector
             pair = dnu[:, rows(s), 0:NC].rearrange("p n (c g) -> p n c g", g=2)
             ps = sum_pool.tile([P, ST, P], F32, name="ps")
+            live[("ps", s)] = ps
             eng.tensor_tensor(out=ps[:], in0=pair[:, :, :, 0], in1=pair[:, :, :, 1], op=ALU.add)
+
+        def log_scale(s):
+            ps = live[("ps", s)]
             sc = out_pool.tile([P, ST, P], F32, name="sc")
-            nc.vector.tensor_tensor(
+            eng2 = nc.gpsimd if POOL_P2 else nc.vector
+            eng2.tensor_tensor(
                 out=split_i(sc[:]), in0=split_i(ps[:]), in1=over_i(ke, s, 16), op=ALU.add
             )
             nc.sync.dma_start(out=sc_v[:, rows(s), :], in_=sc[:])
@@ -311,28 +341,63 @@ def tile_chainlveg_pa_t_kernel(
                 if i < len(second):
                     second[i][0](*second[i][1])
 
-        for step in range(-2, len(GROUPS) + 1):
-            weave(
-                [(back_transpose, (s, tl)) for s in members(step) for tl in range(ST)],
-                [(project, (s, cb)) for s in members(step + 1) for cb in (2, 3, 0, 1)],
-            )
-            for s in members(step - 1):
-                half_terms(s)
-            weave(
-                [(x_transpose, (s, h)) for s in members(step + 2) for h in range(2)],
-                [(variance, (s, h)) for s in members(step - 1) for h in range(2)],
-            )
-            for s in members(step - 1):
-                log_scale(s)
-            for s in members(step + 2):
+        def do_bt(gi):
+            for s in members(gi):
+                for tl in range(ST):
+                    back_transpose(s, tl)
+                    if POOL_DA:
+                        scaled_diff_tile(s, tl)
+
+        def do_q(gi):
+            for s in members(gi):
                 x_quantise(s)
-            if step == -2:
-                prepare_state()
-            for s in members(step):
-                sigmoid(s)
-            for s in members(step):
-                gain(s)
-            for s in members(step):
-                mean(s)
-            for s in members(step):
+
+        def do_ln(gi):
+            for s in members(gi):
                 log_weight(s)
+
+        def do_va(gi):
+            for s in members(gi):
+                for h in range(2):
+                    variance(s, h)
+
+        def do_es(gi):
+            for s in members(gi):
+                half_terms(s)
+            for s in members(gi):
+                pair_sum(s)
+
+        def do_p2(gi):
+            for s in members(gi):
+                log_scale(s)
+
+        def do_sg(gi):
+            for s in members(gi):
+                sigmoid(s)
+
+        def do_mm(gi):
+            for s in members(gi):
+                for cb in (2, 3, 0, 1):
+                    project(s, cb)
+
+        def do_xt(gi):
+            for s in members(gi):
+                for h in range(2):
+                    x_transpose(s, h)
+            if gi == 0:
+                bias_columns()
+
+        def do_ms(gi):
+            for s in members(gi):
+                gain(s)
+            for s in members(gi):
+                mean(s)
+
+        table = {"bt": do_bt, "q": do_q, "ln": do_ln, "es": do_es, "sg": do_sg, "mm": do_mm,
+                 "xt": do_xt, "ms": do_ms, "va": do_va, "p2": do_p2}
+        prepare_state()
+        prepare_rest()
+        prepare_weights()
+        for step in range(-4, len(GROUPS) + 3):
+            for what, lag in PLAN:
+                table[what](step + lag)

@@ -20,7 +20,7 @@ ST = 4
 K = 512
 NC = 256
 GROUPS = ((0,), (1,), (2,), (3,), (4,), (5,), (6,), (7,))
-POOL_DA = True
+POOL_DA = False
 POOL_P1 = False
 POOL_P2 = False
 RING = {"grp": 2, "xq": 2, "y1m": 2, "y1v": 2, "y2v": 4, "da": 3, "out": 3, "sum": 2}

@@ -16,15 +16,18 @@ FLOPS = 2 * 4096 * 512 * 512
 
 P = 128
 NT = 32
-ST = 4
 K = 512
 NC = 256
-GROUPS = ((0,), (1,), (2,), (3,), (4,), (5,), (6,), (7,))
-POOL_DA = False
+SIZES = (4, 4, 4, 4, 4, 4, 4, 4)
+PERIODS = ((0, 1, 2, 3, 4, 5, 6, 7),)
+LEAD = 2
+XL = 3
+QL = 2
+ML = 1
+POOL_DA = True
+POOL_HL = False
 POOL_P1 = False
-POOL_P2 = False
-RING = {"grp": 2, "xq": 2, "y1m": 2, "y1v": 2, "y2v": 4, "da": 3, "out": 3, "sum": 2}
-PLAN = (("q", 2), ("ln", -1), ("xt", 3), ("bt", 1), ("va", -1), ("mm", 2), ("ms", 0), ("sg", 1), ("es", -1), ("p2", -1))
+RING = {"grp": 2, "xq": 3, "y1m": 2, "y1v": 8, "da": 3, "out": 3, "sum": 2}
 
 
 def tile_chainlveg_pa_t_kernel(
@@ -38,19 +41,24 @@ def tile_chainlveg_pa_t_kernel(
     smu_v = s_mu.rearrange("b (c n) j e g -> (b c) (n j e g)", n=NT)
     svar_v = s_var.rearrange("b (c n) j e g -> (b c) (n j e g)", n=NT)
     sw_v = s_weight.rearrange("b (c n) j e -> (b c) (n j e)", n=NT)
+    units = len(SIZES)
+    first = [sum(SIZES[:s]) for s in range(units)]
+    big = max(SIZES)
 
     with ExitStack() as ctx:
         const = ctx.enter_context(tc.tile_pool(name="const", bufs=1))
         grp_pool = ctx.enter_context(tc.tile_pool(name="grp", bufs=RING["grp"]))
         xq_pool = ctx.enter_context(tc.tile_pool(name="xq", bufs=RING["xq"]))
         y1m_pool = ctx.enter_context(tc.tile_pool(name="y1m", bufs=RING["y1m"]))
-        da_pool = ctx.enter_context(tc.tile_pool(name="da", bufs=RING["da"]))
         y1v_pool = ctx.enter_context(tc.tile_pool(name="y1v", bufs=RING["y1v"]))
-        y2v_pool = ctx.enter_context(tc.tile_pool(name="y2v", bufs=RING["y2v"]))
+        da_pool = ctx.enter_context(tc.tile_pool(name="da", bufs=RING["da"]))
         out_pool = ctx.enter_context(tc.tile_pool(name="outp", bufs=RING["out"]))
         sum_pool = ctx.enter_context(tc.tile_pool(name="sump", bufs=RING["sum"]))
         psum = ctx.enter_context(tc.psum_pool(name="psum", bufs=4))
         ctx.enter_context(tc.manual_schedule())
+
+        def rows(s):
+            return slice(first[s], first[s] + SIZES[s])
 
         x_sb = const.tile([P, NT, K], BF16, name="x_sb")
         wraw = const.tile([P, 4, 2 * NC], BF16, name="wraw")
@@ -60,46 +68,29 @@ def tile_chainlveg_pa_t_kernel(
         sw = const.tile([P, NT * 8], BF16, name="sw")
         nc.vector.memset(bz[:], 0.0)
         nc.scalar.dma_start(out=svar[:], in_=svar_v)
-        nc.sync.dma_start(out=x_sb[:, 0:ST, :], in_=xv[:, 0:ST, :])
+        nc.sync.dma_start(out=x_sb[:, rows(0), :], in_=xv[:, rows(0), :])
         nc.scalar.dma_start(out=smu[:], in_=smu_v)
-        nc.scalar.dma_start(out=sw[:], in_=sw_v)
-        nc.scalar.dma_start(out=bz[0:2, :], in_=tcm_b.rearrange("(r c) -> r c", r=2))
-        nc.scalar.dma_start(out=bz[2:4, :], in_=tcv_b.rearrange("(r c) -> r c", r=2))
         for u in range(2):
             for w, off in ((tcm_w, 0), (tcv_w, NC)):
                 nc.sync.dma_start(
                     out=wraw[:, 2 * u : 2 * u + 2, off : off + NC],
                     in_=w[256 * u : 256 * u + 256, :].rearrange("(q e) c -> q e c", e=2),
                 )
-        nc.sync.dma_start(out=x_sb[:, ST : 2 * ST, :], in_=xv[:, ST : 2 * ST, :])
-        for s in range(2, NT // ST):
-            nc.sync.dma_start(
-                out=x_sb[:, s * ST : (s + 1) * ST, :], in_=xv[:, s * ST : (s + 1) * ST, :]
-            )
+        nc.scalar.dma_start(out=sw[:], in_=sw_v)
+        nc.scalar.dma_start(out=bz[0:2, :], in_=tcm_b.rearrange("(r c) -> r c", r=2))
+        nc.scalar.dma_start(out=bz[2:4, :], in_=tcv_b.rearrange("(r c) -> r c", r=2))
+        for s in range(1, units):
+            nc.sync.dma_start(out=x_sb[:, rows(s), :], in_=xv[:, rows(s), :])
 
         ident = const.tile([P, P], F32, name="ident")
         masks.make_identity(nc, ident[:])
-        two = const.tile([P, 1], F32, name="two")
-        nc.vector.memset(two[:], 2.0)
-
+        minus = const.tile([P, 1], F32, name="minus")
+        nc.vector.memset(minus[:], -1.0)
         wgrp = const.tile([P, 2 * NC, 4], BF16, name="wgrp", align_bytes=64)
         wq = const.tile([P, 2 * NC], U32, name="wq", align_bytes=64)
         wsc = const.tile([P, 2 * NC], U8, name="wsc", align_bytes=64)
         bf = const.tile([P, P], F32, name="bf")
         b1 = const.tile([P, 4], F32, name="b1")
-
-        def prepare_weights():
-            nc.vector.tensor_copy(out=wgrp[:], in_=wraw[:].rearrange("p t c -> p c t"))
-            nc.vector.tensor_copy(out=bf[:], in_=bz[:])
-            nc.vector.quantize_mx(
-                out=wq[:].bitcast(FP8X4), scales=wsc[:], in_=wgrp[:].rearrange("p c t -> p (c t)")
-            )
-
-        def bias_columns():
-            bt = psum.tile([P, 512], F32, name="bt", tag="pa")
-            nc.tensor.transpose(bt[:, 0:P], bf[:], ident[:])
-            nc.vector.tensor_scalar_add(out=b1[:], in0=bt[:, 0:4], scalar1=1.0)
-
         dnu = const.tile([P, NT, 2 * NC], F32, name="dnu")
         m1e = const.tile([P, NT, 32], F32, name="m1e")
         m1p = const.tile([P, NT, 32], F32, name="m1p")
@@ -110,6 +101,7 @@ def tile_chainlveg_pa_t_kernel(
         ke = const.tile([P, NT, 16], F32, name="ke")
 
         live = {}
+        done = set()
 
         def spread(small):
             return (
@@ -123,20 +115,18 @@ def tile_chainlveg_pa_t_kernel(
             return full[:].rearrange("p n (j t g) -> p (n j) t g", t=2, g=2)
 
         def prepare_state():
-            nc.vector.tensor_scalar(
-                out=as_njtg(v1p), in0=spread(svar), scalar1=-1.0, scalar2=1.0,
-                op0=ALU.mult, op1=ALU.add,
-            )
+            nc.scalar.activation(out=as_njtg(hae), in_=spread(svar), func=ACT.Exp, scale=-2.0)
+            nc.vector.tensor_scalar_add(out=as_njtg(v1p), in0=spread(svar), scalar1=1.0)
             nc.vector.tensor_copy(out=as_njtg(m1e), in_=spread(smu))
             nc.vector.tensor_scalar_add(out=m1p[:], in0=m1e[:], scalar1=1.0)
+            nc.vector.tensor_copy(out=bf[:], in_=bz[:])
+            nc.vector.tensor_scalar_mul(out=hae[:], in0=hae[:], scalar1=0.5)
 
         def prepare_rest():
-            nc.scalar.activation(out=as_njtg(hae), in_=spread(svar), func=ACT.Exp, scale=-2.0)
-            nc.vector.tensor_scalar_mul(out=hae[:], in0=hae[:], scalar1=0.5)
             pairs = svar[:].rearrange("p (a g) -> p a g", g=2)
             nc.vector.tensor_tensor(out=vs[:], in0=pairs[:, :, 0], in1=pairs[:, :, 1], op=ALU.add)
             nc.vector.scalar_tensor_tensor(
-                out=k0[:], in0=sw[:], scalar=-(math.log(2.0 * math.pi) + 2.0), in1=vs[:],
+                out=k0[:], in0=sw[:], scalar=2.0 - math.log(2.0 * math.pi), in1=vs[:],
                 op0=ALU.add, op1=ALU.subtract,
             )
             nc.vector.tensor_copy(
@@ -144,260 +134,280 @@ def tile_chainlveg_pa_t_kernel(
                 in_=k0[:].unsqueeze(2).to_broadcast([P, NT * 8, 2]),
             )
 
-        def x_transpose(s, h):
-            if h == 0:
-                live[("grp", s)] = grp_pool.tile([P, 4 * 512], BF16, name="grp", align_bytes=64)
-            grp = live[("grp", s)]
-            xt = psum.tile([P, 2, 256], F32, name="xt", tag="pa")
-            for j in range(2):
-                words = x_sb[:, s * ST + 2 * h + j, :].bitcast(F32)
-                for u in range(2):
-                    nc.tensor.transpose(
-                        xt[:, u, j * P : (j + 1) * P], words[:, u * P : (u + 1) * P], ident[:]
-                    )
-            nc.scalar.copy(
-                out=grp[:].bitcast(F32)[:, h * 512 : (h + 1) * 512].rearrange(
-                    "p (r u) -> p r u", u=2
-                ),
-                in_=xt[:].rearrange("p u r -> p r u"),
+        def prepare_weights():
+            nc.vector.tensor_copy(out=wgrp[:], in_=wraw[:].rearrange("p t c -> p c t"))
+            nc.vector.quantize_mx(
+                out=wq[:].bitcast(FP8X4), scales=wsc[:], in_=wgrp[:].rearrange("p c t -> p (c t)")
             )
+
+        def bias_columns():
+            bt = psum.tile([P, 512], F32, name="bt", tag="pa")
+            nc.tensor.transpose(bt[:, 0:P], bf[:], ident[:])
+            nc.vector.tensor_scalar_add(out=b1[:], in0=bt[:, 0:4], scalar1=1.0)
+
+        def x_transpose(s):
+            done.add(("xt", s))
+            size = SIZES[s]
+            grp = grp_pool.tile([P, 4 * P * big], BF16, name="grp", align_bytes=64)
+            live[("grp", s)] = grp
+            for lo in range(0, size, 2):
+                cnt = min(2, size - lo)
+                xt = psum.tile([P, 2, 2 * P], F32, name="xt", tag="pa")
+                for j in range(cnt):
+                    words = x_sb[:, first[s] + lo + j, :].bitcast(F32)
+                    for u in range(2):
+                        nc.tensor.transpose(
+                            xt[:, u, j * P : (j + 1) * P], words[:, u * P : (u + 1) * P], ident[:]
+                        )
+                nc.scalar.copy(
+                    out=grp[:].bitcast(F32)[:, lo * 2 * P : (lo + cnt) * 2 * P].rearrange(
+                        "p (r u) -> p r u", u=2
+                    ),
+                    in_=xt[:, :, 0 : cnt * P].rearrange("p u r -> p r u"),
+                )
 
         def x_quantise(s):
-            xq = xq_pool.tile([P, 512], U32, name="xq", align_bytes=64)
-            xs = xq_pool.tile([P, 512], U8, name="xs", align_bytes=64)
+            assert ("xt", s) in done
+            done.add(("q", s))
+            wide = P * SIZES[s]
+            xq = xq_pool.tile([P, P * big], U32, name="xq", align_bytes=64)
+            xs = xq_pool.tile([P, P * big], U8, name="xs", align_bytes=64)
             live[("xq", s)] = (xq, xs)
             nc.vector.quantize_mx(
-                out=xq[:].bitcast(FP8X4), scales=xs[:], in_=live[("grp", s)][:]
+                out=xq[:, 0:wide].bitcast(FP8X4), scales=xs[:, 0:wide],
+                in_=live[("grp", s)][:, 0 : 4 * wide],
             )
 
-        def project(s, cb):
+        def project(s):
+            assert ("q", s) in done
+            done.add(("mm", s))
+            wide = P * SIZES[s]
             xq, xs = live[("xq", s)]
-            if cb == 2:
-                live[("y1v", s)] = y1v_pool.tile([P, 2, 512], F32, name="y1v")
-            if cb == 0:
-                live[("y1m", s)] = y1m_pool.tile([P, 2, 512], F32, name="y1m")
-            pc = psum.tile([P, 512], F32, name="pc", tag="pa")
-            nc.tensor.matmul_mx(
-                out=pc[:],
-                lhsT=wq[:, cb * P : (cb + 1) * P].bitcast(FP8X4),
-                lhsT_scale=wsc[:, cb * P : (cb + 1) * P],
-                rhs=xq[:].bitcast(FP8X4),
-                rhs_scale=xs[:],
-                start=True,
-                stop=True,
+            y1 = (
+                y1m_pool.tile([P, 2, P * big], F32, name="y1m"),
+                y1v_pool.tile([P, 2, P * big], F32, name="y1v"),
             )
-            dest = live[("y1m", s)][:, cb, :] if cb < 2 else live[("y1v", s)][:, cb - 2, :]
-            nc.scalar.activation(
-                out=dest, in_=pc[:], func=ACT.Relu, bias=b1[:, cb : cb + 1], scale=1.0
-            )
-            if cb == 3:
-                y2v = y2v_pool.tile([P, 2, 512], F32, name="y2v")
-                live[("y2v", s)] = y2v
+            live[("y1", s)] = y1
+            for cb in range(4):
+                pc = psum.tile([P, 512], F32, name="pc", tag="pa")
+                nc.tensor.matmul_mx(
+                    out=pc[:, 0:wide],
+                    lhsT=wq[:, cb * P : (cb + 1) * P].bitcast(FP8X4),
+                    lhsT_scale=wsc[:, cb * P : (cb + 1) * P],
+                    rhs=xq[:, 0:wide].bitcast(FP8X4),
+                    rhs_scale=xs[:, 0:wide],
+                    start=True,
+                    stop=True,
+                )
                 nc.scalar.activation(
-                    out=y2v[:], in_=live[("y1v", s)][:], func=ACT.Relu, bias=two[:], scale=-1.0
+                    out=y1[cb // 2][:, cb % 2, 0:wide], in_=pc[:, 0:wide], func=ACT.Relu,
+                    bias=b1[:, cb : cb + 1], scale=1.0,
                 )
 
-        def back_transpose(s, tl):
-            n = s * ST + tl
-            y1m = live[("y1m", s)]
-            y2v = live[("y2v", s)]
-            yt = psum.tile([P, 512], F32, name="yt", tag="pv")
-            for cb in range(2):
-                nc.tensor.transpose(
-                    yt[:, cb * P : (cb + 1) * P], y1m[:, cb, tl * P : (tl + 1) * P], ident[:]
-                )
-            for cb in range(2):
-                nc.tensor.transpose(
-                    yt[:, NC + cb * P : NC + (cb + 1) * P],
-                    y2v[:, cb, tl * P : (tl + 1) * P],
-                    ident[:],
-                )
-            nc.vector.scalar_tensor_tensor(
-                out=dnu[:, n, 0:NC].rearrange("p (i c) -> p i c", i=8),
-                in0=yt[:, 0:NC].rearrange("p (i c) -> p i c", i=8),
-                scalar=2.0,
-                in1=m1p[:, n, :].unsqueeze(1).to_broadcast([P, 8, 32]),
-                op0=ALU.min,
-                op1=ALU.subtract,
-            )
-            nc.vector.tensor_tensor(
-                out=dnu[:, n, NC : 2 * NC].rearrange("p (i c) -> p i c", i=8),
-                in0=yt[:, NC : 2 * NC].rearrange("p (i c) -> p i c", i=8),
-                in1=v1p[:, n, :].unsqueeze(1).to_broadcast([P, 8, 32]),
-                op=ALU.subtract,
-            )
+        def by_i(ap):
+            return ap.rearrange("p (i c) -> p i c", i=8)
 
-        def rows(s):
-            return slice(s * ST, (s + 1) * ST)
+        def back_transpose(s):
+            assert ("mm", s) in done
+            done.add(("bt", s))
+            y1 = live[("y1", s)]
+            if POOL_DA:
+                live[("da", s)] = da_pool.tile([P, big, NC], F32, name="da")
+            for tl in range(SIZES[s]):
+                n = first[s] + tl
+                yt = psum.tile([P, 512], F32, name="yt", tag="pv")
+                for cb in range(4):
+                    nc.tensor.transpose(
+                        yt[:, cb * P : (cb + 1) * P],
+                        y1[cb // 2][:, cb % 2, tl * P : (tl + 1) * P],
+                        ident[:],
+                    )
+                for half, small in ((0, m1p), (1, v1p)):
+                    nc.vector.scalar_tensor_tensor(
+                        out=by_i(dnu[:, n, half * NC : (half + 1) * NC]),
+                        in0=by_i(yt[:, half * NC : (half + 1) * NC]),
+                        scalar=2.0,
+                        in1=small[:, n, :].unsqueeze(1).to_broadcast([P, 8, 32]),
+                        op0=ALU.min,
+                        op1=ALU.subtract,
+                    )
+                if POOL_DA:
+                    nc.gpsimd.tensor_tensor(
+                        out=by_i(live[("da", s)][:, tl, :]),
+                        in0=by_i(dnu[:, n, 0:NC]),
+                        in1=hae[:, n, :].unsqueeze(1).to_broadcast([P, 8, 32]),
+                        op=ALU.mult,
+                    )
 
         def over_i(small, s, width):
-            return small[:, rows(s), :].unsqueeze(2).to_broadcast([P, ST, 8, width])
+            return small[:, rows(s), :].unsqueeze(2).to_broadcast([P, SIZES[s], 8, width])
 
         def split_i(ap):
             return ap.rearrange("p n (i c) -> p n i c", i=8)
 
-        def scaled_diff(s):
-            da = da_pool.tile([P, ST, NC], F32, name="da")
-            live[("da", s)] = da
-            nc.vector.tensor_tensor(
-                out=split_i(da[:]), in0=split_i(dnu[:, rows(s), 0:NC]), in1=over_i(hae, s, 32),
-                op=ALU.mult,
-            )
-
-        def scaled_diff_tile(s, tl):
-            if tl == 0:
-                live[("da", s)] = da_pool.tile([P, ST, NC], F32, name="da")
-            n = s * ST + tl
-            nc.gpsimd.tensor_tensor(
-                out=live[("da", s)][:, tl, :].rearrange("p (i c) -> p i c", i=8),
-                in0=dnu[:, n, 0:NC].rearrange("p (i c) -> p i c", i=8),
-                in1=hae[:, n, :].unsqueeze(1).to_broadcast([P, 8, 32]),
-                op=ALU.mult,
-            )
-
         def sigmoid(s):
-            nu = dnu[:, rows(s), NC : 2 * NC]
-            nc.scalar.activation(out=nu, in_=nu, func=ACT.Sigmoid, scale=2.0)
+            assert ("bt", s) in done
+            done.add(("sg", s))
+            u = dnu[:, rows(s), NC : 2 * NC]
+            nc.scalar.activation(out=u, in_=u, func=ACT.Sigmoid, scale=-2.0)
 
         def gain(s):
-            g = out_pool.tile([P, ST, NC], F32, name="gmu")
+            assert ("sg", s) in done
+            done.add(("g", s))
+            g = out_pool.tile([P, big, NC], F32, name="gmu")
             live[("g", s)] = g
             nc.vector.tensor_tensor(
-                out=g[:], in0=dnu[:, rows(s), 0:NC], in1=dnu[:, rows(s), NC : 2 * NC], op=ALU.mult
+                out=g[:, 0 : SIZES[s], :], in0=dnu[:, rows(s), 0:NC],
+                in1=dnu[:, rows(s), NC : 2 * NC], op=ALU.mult,
             )
 
         def mean(s):
-            g = live[("g", s)]
+            assert ("g", s) in done
+            done.add(("ms", s))
+            g = live[("g", s)][:, 0 : SIZES[s], :]
             dn = dnu[:, rows(s), 0:NC]
             if not POOL_DA:
-                scaled_diff(s)
-            nc.vector.tensor_tensor(out=dn, in0=g[:], in1=live[("da", s)][:], op=ALU.mult)
+                live[("da", s)] = da_pool.tile([P, big, NC], F32, name="da")
+                nc.vector.tensor_tensor(
+                    out=split_i(live[("da", s)][:, 0 : SIZES[s], :]), in0=split_i(dn),
+                    in1=over_i(hae, s, 32), op=ALU.mult,
+                )
             nc.vector.tensor_tensor(
-                out=split_i(g[:]), in0=split_i(g[:]), in1=over_i(m1e, s, 32), op=ALU.add
+                out=dn, in0=g, in1=live[("da", s)][:, 0 : SIZES[s], :], op=ALU.mult
             )
-            nc.sync.dma_start(out=mu_v[:, rows(s), :], in_=g[:])
+            nc.vector.tensor_tensor(
+                out=split_i(g), in0=split_i(g), in1=over_i(m1e, s, 32), op=ALU.add
+            )
+            nc.sync.dma_start(out=mu_v[:, rows(s), :], in_=g)
 
         def log_weight(s):
+            assert ("g", s) in done
+            done.add(("ln", s))
             wc = dnu[:, rows(s), NC : 2 * NC]
-            nc.scalar.activation(out=wc, in_=wc, func=ACT.Ln, scale=math.exp(2.0))
+            nc.scalar.activation(out=wc, in_=wc, func=ACT.Ln)
+            if POOL_HL:
+                for lo in range(first[s], first[s] + SIZES[s]):
+                    part = dnu[:, lo : lo + 1, NC : 2 * NC]
+                    nc.gpsimd.tensor_scalar(
+                        out=part, in0=part, scalar1=0.5, scalar2=-1.0, op0=ALU.mult, op1=ALU.add
+                    )
+            else:
+                nc.scalar.activation(out=wc, in_=wc, func=ACT.Identity, bias=minus[:], scale=0.5)
+
+        def variance(s):
+            assert ("ln", s) in done
+            done.add(("va", s))
+            size = SIZES[s]
+            vt = out_pool.tile([P, big, NC], F32, name="var")
+            y1 = live[("y1", s)]
+            for lo in range(0, size, 2):
+                cnt = min(2, size - lo)
+                yv = psum.tile([P, 2, NC], F32, name="yv", tag="pv")
+                for j in range(cnt):
+                    tl = lo + j
+                    for cb in range(2):
+                        nc.tensor.transpose(
+                            yv[:, j, cb * P : (cb + 1) * P],
+                            y1[1][:, cb, tl * P : (tl + 1) * P],
+                            ident[:],
+                        )
+                n = first[s] + lo
+                nc.vector.scalar_tensor_tensor(
+                    out=vt[:, lo : lo + cnt, :],
+                    in0=yv[:, 0:cnt, :],
+                    scalar=2.0,
+                    in1=dnu[:, n : n + cnt, NC : 2 * NC],
+                    op0=ALU.min,
+                    op1=ALU.add,
+                )
+            nc.sync.dma_start(out=var_v[:, rows(s), :], in_=vt[:, 0:size, :])
 
         def half_terms(s):
-            nc.vector.scalar_tensor_tensor(
-                out=dnu[:, rows(s), 0:NC],
-                in0=dnu[:, rows(s), NC : 2 * NC],
-                scalar=0.5,
-                in1=dnu[:, rows(s), 0:NC],
-                op0=ALU.mult,
-                op1=ALU.subtract,
+            assert ("ln", s) in done and ("ms", s) in done
+            done.add(("lq", s))
+            nc.vector.tensor_tensor(
+                out=dnu[:, rows(s), 0:NC], in0=dnu[:, rows(s), NC : 2 * NC],
+                in1=dnu[:, rows(s), 0:NC], op=ALU.subtract,
             )
-
-        def variance(s, h):
-            if h == 0:
-                live[("var", s)] = out_pool.tile([P, ST, NC], F32, name="var")
-            vt = live[("var", s)]
-            y2v = live[("y2v", s)]
-            yv = psum.tile([P, 2, NC], F32, name="yv", tag="pv")
-            for j in range(2):
-                tl = 2 * h + j
-                for cb in range(2):
-                    nc.tensor.transpose(
-                        yv[:, j, cb * P : (cb + 1) * P], y2v[:, cb, tl * P : (tl + 1) * P], ident[:]
-                    )
-            n = s * ST + 2 * h
-            nc.vector.scalar_tensor_tensor(
-                out=vt[:, 2 * h : 2 * h + 2, :],
-                in0=dnu[:, n : n + 2, NC : 2 * NC],
-                scalar=0.5,
-                in1=yv[:],
-                op0=ALU.mult,
-                op1=ALU.subtract,
-            )
-            if h == 1:
-                nc.sync.dma_start(out=var_v[:, rows(s), :], in_=vt[:])
-
-        def pair_sum(s):
             eng = nc.gpsimd if POOL_P1 else nc.vector
             pair = dnu[:, rows(s), 0:NC].rearrange("p n (c g) -> p n c g", g=2)
-            ps = sum_pool.tile([P, ST, P], F32, name="ps")
+            ps = sum_pool.tile([P, big, P], F32, name="ps")
             live[("ps", s)] = ps
-            eng.tensor_tensor(out=ps[:], in0=pair[:, :, :, 0], in1=pair[:, :, :, 1], op=ALU.add)
+            eng.tensor_tensor(
+                out=ps[:, 0 : SIZES[s], :], in0=pair[:, :, :, 0], in1=pair[:, :, :, 1], op=ALU.add
+            )
 
         def log_scale(s):
-            ps = live[("ps", s)]
-            sc = out_pool.tile([P, ST, P], F32, name="sc")
-            eng2 = nc.gpsimd if POOL_P2 else nc.vector
-            eng2.tensor_tensor(
-                out=split_i(sc[:]), in0=split_i(ps[:]), in1=over_i(ke, s, 16), op=ALU.add
+            assert ("lq", s) in done
+            ps = live[("ps", s)][:, 0 : SIZES[s], :]
+            sc = out_pool.tile([P, big, P], F32, name="sc")
+            nc.vector.tensor_tensor(
+                out=split_i(sc[:, 0 : SIZES[s], :]), in0=split_i(ps), in1=over_i(ke, s, 16),
+                op=ALU.add,
             )
-            nc.sync.dma_start(out=sc_v[:, rows(s), :], in_=sc[:])
+            nc.sync.dma_start(out=sc_v[:, rows(s), :], in_=sc[:, 0 : SIZES[s], :])
 
-        def members(gi):
-            return GROUPS[gi] if 0 <= gi < len(GROUPS) else ()
+        period_of = {}
+        for index, period in enumerate(PERIODS):
+            for s in period:
+                period_of[s] = index
+        issued = {"sg": set(), "ln": set()}
+        held = {"sg": [], "ln": []}
 
-        def weave(first, second):
-            for i in range(max(len(first), len(second))):
-                if i < len(first):
-                    first[i][0](*first[i][1])
-                if i < len(second):
-                    second[i][0](*second[i][1])
+        def may_run(kind, s):
+            index = period_of[s]
+            if kind == "sg":
+                return index == 0 or all(v in issued["ln"] for v in PERIODS[index - 1])
+            return all(v in issued["sg"] for v in PERIODS[index])
 
-        def do_bt(gi):
-            for s in members(gi):
-                for tl in range(ST):
-                    back_transpose(s, tl)
-                    if POOL_DA:
-                        scaled_diff_tile(s, tl)
+        def table_work(kind, s):
+            held[kind] = held[kind] + [s]
+            moved = True
+            while moved:
+                moved = False
+                for k2, work in (("sg", sigmoid), ("ln", log_weight)):
+                    for v in held[k2]:
+                        if may_run(k2, v):
+                            work(v)
+                            issued[k2].add(v)
+                            moved = True
+                    held[k2] = [v for v in held[k2] if v not in issued[k2]]
 
-        def do_q(gi):
-            for s in members(gi):
-                x_quantise(s)
+        def front(s):
+            if 0 <= s < units:
+                back_transpose(s)
+            if 0 <= s + QL < units:
+                x_quantise(s + QL)
+            if s == 0:
+                prepare_rest()
+            if 0 <= s + ML < units:
+                project(s + ML)
+            if 0 <= s + XL < units:
+                x_transpose(s + XL)
+                if s + XL == 0:
+                    bias_columns()
+            if 0 <= s < units:
+                table_work("sg", s)
 
-        def do_ln(gi):
-            for s in members(gi):
-                log_weight(s)
+        def products(s):
+            gain(s)
+            table_work("ln", s)
+            mean(s)
 
-        def do_va(gi):
-            for s in members(gi):
-                for h in range(2):
-                    variance(s, h)
+        def logs(s):
+            variance(s)
+            half_terms(s)
+            log_scale(s)
 
-        def do_es(gi):
-            for s in members(gi):
-                half_terms(s)
-            for s in members(gi):
-                pair_sum(s)
-
-        def do_p2(gi):
-            for s in members(gi):
-                log_scale(s)
-
-        def do_sg(gi):
-            for s in members(gi):
-                sigmoid(s)
-
-        def do_mm(gi):
-            for s in members(gi):
-                for cb in (2, 3, 0, 1):
-                    project(s, cb)
-
-        def do_xt(gi):
-            for s in members(gi):
-                for h in range(2):
-                    x_transpose(s, h)
-            if gi == 0:
-                bias_columns()
-
-        def do_ms(gi):
-            for s in members(gi):
-                gain(s)
-            for s in members(gi):
-                mean(s)
-
-        table = {"bt": do_bt, "q": do_q, "ln": do_ln, "es": do_es, "sg": do_sg, "mm": do_mm,
-                 "xt": do_xt, "ms": do_ms, "va": do_va, "p2": do_p2}
+        jobs = []
+        for period in PERIODS:
+            jobs.extend([(products, s) for s in period])
+            jobs.extend([(logs, s) for s in period])
         prepare_state()
-        prepare_rest()
         prepare_weights()
-        for step in range(-4, len(GROUPS) + 3):
-            for what, lag in PLAN:
-                table[what](step + lag)
+        for s in range(-XL, LEAD):
+            front(s)
+        for index, job in enumerate(jobs):
+            job[0](job[1])
+            if index + LEAD < units:
+                front(index + LEAD)

@@ -21,12 +21,15 @@ NC = 256
 SIZES = (4, 4, 4, 4, 4, 4, 4, 4)
 PERIODS = ((0, 1, 2, 3, 4, 5, 6, 7),)
 LEAD = 2
+SPLIT = 2
+MFIRST = True
+PIPE_ES = True
 XL = 3
 QL = 2
 ML = 1
 POOL_DA = True
 POOL_HL = False
-POOL_P1 = False
+POOL_P1 = True
 RING = {"grp": 2, "xq": 3, "y1m": 2, "y1v": 8, "da": 3, "out": 3, "sum": 2}
 
 
@@ -213,24 +216,32 @@ def tile_chainlveg_pa_t_kernel(
             y1 = live[("y1", s)]
             if POOL_DA:
                 live[("da", s)] = da_pool.tile([P, big, NC], F32, name="da")
+            banks = []
+
+            def clip_and_subtract(tl, half, small):
+                n = first[s] + tl
+                nc.vector.scalar_tensor_tensor(
+                    out=by_i(dnu[:, n, half * NC : (half + 1) * NC]),
+                    in0=by_i(banks[tl][:, half * NC : (half + 1) * NC]),
+                    scalar=2.0,
+                    in1=small[:, n, :].unsqueeze(1).to_broadcast([P, 8, 32]),
+                    op0=ALU.min,
+                    op1=ALU.subtract,
+                )
+
             for tl in range(SIZES[s]):
                 n = first[s] + tl
                 yt = psum.tile([P, 512], F32, name="yt", tag="pv")
+                banks.append(yt)
                 for cb in range(4):
                     nc.tensor.transpose(
                         yt[:, cb * P : (cb + 1) * P],
                         y1[cb // 2][:, cb % 2, tl * P : (tl + 1) * P],
                         ident[:],
                     )
-                for half, small in ((0, m1p), (1, v1p)):
-                    nc.vector.scalar_tensor_tensor(
-                        out=by_i(dnu[:, n, half * NC : (half + 1) * NC]),
-                        in0=by_i(yt[:, half * NC : (half + 1) * NC]),
-                        scalar=2.0,
-                        in1=small[:, n, :].unsqueeze(1).to_broadcast([P, 8, 32]),
-                        op0=ALU.min,
-                        op1=ALU.subtract,
-                    )
+                clip_and_subtract(tl, 0, m1p)
+                if not MFIRST:
+                    clip_and_subtract(tl, 1, v1p)
                 if POOL_DA:
                     nc.gpsimd.tensor_tensor(
                         out=by_i(live[("da", s)][:, tl, :]),
@@ -238,9 +249,16 @@ def tile_chainlveg_pa_t_kernel(
                         in1=hae[:, n, :].unsqueeze(1).to_broadcast([P, 8, 32]),
                         op=ALU.mult,
                     )
+            if MFIRST:
+                for tl in range(SIZES[s]):
+                    clip_and_subtract(tl, 1, v1p)
 
-        def over_i(small, s, width):
-            return small[:, rows(s), :].unsqueeze(2).to_broadcast([P, SIZES[s], 8, width])
+        def pieces(s):
+            step = max(1, SIZES[s] // SPLIT)
+            return [(lo, min(step, SIZES[s] - lo)) for lo in range(0, SIZES[s], step)]
+
+        def over_i(small, n, cnt, width):
+            return small[:, n : n + cnt, :].unsqueeze(2).to_broadcast([P, cnt, 8, width])
 
         def split_i(ap):
             return ap.rearrange("p n (i c) -> p n i c", i=8)
@@ -256,29 +274,39 @@ def tile_chainlveg_pa_t_kernel(
             done.add(("g", s))
             g = out_pool.tile([P, big, NC], F32, name="gmu")
             live[("g", s)] = g
-            nc.vector.tensor_tensor(
-                out=g[:, 0 : SIZES[s], :], in0=dnu[:, rows(s), 0:NC],
-                in1=dnu[:, rows(s), NC : 2 * NC], op=ALU.mult,
-            )
+            for lo, cnt in pieces(s):
+                n = first[s] + lo
+                nc.vector.tensor_tensor(
+                    out=g[:, lo : lo + cnt, :], in0=dnu[:, n : n + cnt, 0:NC],
+                    in1=dnu[:, n : n + cnt, NC : 2 * NC], op=ALU.mult,
+                )
 
         def mean(s):
             assert ("g", s) in done
             done.add(("ms", s))
-            g = live[("g", s)][:, 0 : SIZES[s], :]
-            dn = dnu[:, rows(s), 0:NC]
+            g = live[("g", s)]
             if not POOL_DA:
                 live[("da", s)] = da_pool.tile([P, big, NC], F32, name="da")
+                for lo, cnt in pieces(s):
+                    n = first[s] + lo
+                    nc.vector.tensor_tensor(
+                        out=split_i(live[("da", s)][:, lo : lo + cnt, :]),
+                        in0=split_i(dnu[:, n : n + cnt, 0:NC]),
+                        in1=over_i(hae, n, cnt, 32), op=ALU.mult,
+                    )
+            for lo, cnt in pieces(s):
+                n = first[s] + lo
                 nc.vector.tensor_tensor(
-                    out=split_i(live[("da", s)][:, 0 : SIZES[s], :]), in0=split_i(dn),
-                    in1=over_i(hae, s, 32), op=ALU.mult,
+                    out=dnu[:, n : n + cnt, 0:NC], in0=g[:, lo : lo + cnt, :],
+                    in1=live[("da", s)][:, lo : lo + cnt, :], op=ALU.mult,
                 )
-            nc.vector.tensor_tensor(
-                out=dn, in0=g, in1=live[("da", s)][:, 0 : SIZES[s], :], op=ALU.mult
-            )
-            nc.vector.tensor_tensor(
-                out=split_i(g), in0=split_i(g), in1=over_i(m1e, s, 32), op=ALU.add
-            )
-            nc.sync.dma_start(out=mu_v[:, rows(s), :], in_=g)
+            for lo, cnt in pieces(s):
+                n = first[s] + lo
+                nc.vector.tensor_tensor(
+                    out=split_i(g[:, lo : lo + cnt, :]), in0=split_i(g[:, lo : lo + cnt, :]),
+                    in1=over_i(m1e, n, cnt, 32), op=ALU.add,
+                )
+            nc.sync.dma_start(out=mu_v[:, rows(s), :], in_=g[:, 0 : SIZES[s], :])
 
         def log_weight(s):
             assert ("g", s) in done
@@ -325,26 +353,35 @@ def tile_chainlveg_pa_t_kernel(
         def half_terms(s):
             assert ("ln", s) in done and ("ms", s) in done
             done.add(("lq", s))
-            nc.vector.tensor_tensor(
-                out=dnu[:, rows(s), 0:NC], in0=dnu[:, rows(s), NC : 2 * NC],
-                in1=dnu[:, rows(s), 0:NC], op=ALU.subtract,
-            )
-            eng = nc.gpsimd if POOL_P1 else nc.vector
-            pair = dnu[:, rows(s), 0:NC].rearrange("p n (c g) -> p n c g", g=2)
+            for lo, cnt in pieces(s):
+                n = first[s] + lo
+                nc.vector.tensor_tensor(
+                    out=dnu[:, n : n + cnt, 0:NC], in0=dnu[:, n : n + cnt, NC : 2 * NC],
+                    in1=dnu[:, n : n + cnt, 0:NC], op=ALU.subtract,
+                )
+
+        def pair_sum(s):
+            eng = nc.gpsimd if POOL_P1 and s != units - 1 else nc.vector
             ps = sum_pool.tile([P, big, P], F32, name="ps")
             live[("ps", s)] = ps
-            eng.tensor_tensor(
-                out=ps[:, 0 : SIZES[s], :], in0=pair[:, :, :, 0], in1=pair[:, :, :, 1], op=ALU.add
-            )
+            for lo, cnt in pieces(s):
+                n = first[s] + lo
+                pair = dnu[:, n : n + cnt, 0:NC].rearrange("p n (c g) -> p n c g", g=2)
+                eng.tensor_tensor(
+                    out=ps[:, lo : lo + cnt, :], in0=pair[:, :, :, 0], in1=pair[:, :, :, 1],
+                    op=ALU.add,
+                )
 
         def log_scale(s):
             assert ("lq", s) in done
-            ps = live[("ps", s)][:, 0 : SIZES[s], :]
+            ps = live[("ps", s)]
             sc = out_pool.tile([P, big, P], F32, name="sc")
-            nc.vector.tensor_tensor(
-                out=split_i(sc[:, 0 : SIZES[s], :]), in0=split_i(ps), in1=over_i(ke, s, 16),
-                op=ALU.add,
-            )
+            for lo, cnt in pieces(s):
+                n = first[s] + lo
+                nc.vector.tensor_tensor(
+                    out=split_i(sc[:, lo : lo + cnt, :]), in0=split_i(ps[:, lo : lo + cnt, :]),
+                    in1=over_i(ke, n, cnt, 16), op=ALU.add,
+                )
             nc.sync.dma_start(out=sc_v[:, rows(s), :], in_=sc[:, 0 : SIZES[s], :])
 
         period_of = {}
@@ -395,8 +432,19 @@ def tile_chainlveg_pa_t_kernel(
             mean(s)
 
         def logs(s):
-            variance(s)
+            if not PIPE_ES:
+                variance(s)
+                half_terms(s)
+                pair_sum(s)
+                log_scale(s)
+                return
+            period = PERIODS[period_of[s]]
+            if s == period[0]:
+                variance(s)
             half_terms(s)
+            pair_sum(s)
+            if s != period[-1]:
+                variance(s + 1)
             log_scale(s)
 
         jobs = []

@@ -15,447 +15,380 @@ ACT = mybir.ActivationFunctionType
 FLOPS = 2 * 4096 * 512 * 512
 
 P = 128
-NT = 32
+TILES = 32
+UNIT = 4
+UNITS = TILES // UNIT
+ROWS = UNIT * P
 K = 512
 NC = 256
-SIZES = (4, 4, 4, 4, 4, 4, 4, 4)
-PERIODS = ((0, 1, 2, 3, 4, 5, 6, 7),)
-LEAD = 2
-SPLIT = 2
-MFIRST = True
-PIPE_ES = True
-XL = 3
-QL = 2
-ML = 1
-POOL_DA = True
-POOL_HL = False
-POOL_P1 = True
-RING = {"grp": 2, "xq": 3, "y1m": 2, "y1v": 8, "da": 3, "out": 3, "sum": 2}
+NI = 8
+JTG = NC // NI
+JT = JTG // 2
+BLOCKS = 2 * NC // P
+AHEAD_PROJECT = 1
+AHEAD_QUANTISE = 2
+AHEAD_TRANSPOSE = 3
+AHEAD_FRONT = 2
+AHEAD_LN = 2
 
 
 def tile_chainlveg_pa_t_kernel(
     tc, x, s_weight, s_mu, s_var, tcm_w, tcm_b, tcv_w, tcv_b, out_0, out_1, out_2
 ):
     nc = tc.nc
-    xv = x.rearrange("b (c n) k -> (b c) n k", n=NT)
-    sc_v = out_0.rearrange("b (c n) i j t e -> (b c) n (i j t e)", n=NT)
-    mu_v = out_1.rearrange("b (c n) i j t e g -> (b c) n (i j t e g)", n=NT)
-    var_v = out_2.rearrange("b (c n) i j t e g -> (b c) n (i j t e g)", n=NT)
-    smu_v = s_mu.rearrange("b (c n) j e g -> (b c) (n j e g)", n=NT)
-    svar_v = s_var.rearrange("b (c n) j e g -> (b c) (n j e g)", n=NT)
-    sw_v = s_weight.rearrange("b (c n) j e -> (b c) (n j e)", n=NT)
-    units = len(SIZES)
-    first = [sum(SIZES[:s]) for s in range(units)]
-    big = max(SIZES)
+    x_rows = x.rearrange("b (c n) k -> (b c) n k", n=TILES)
+    scale_rows = out_0.rearrange("b (c n) i j t e -> (b c) n (i j t e)", n=TILES)
+    mu_rows = out_1.rearrange("b (c n) i j t e g -> (b c) n (i j t e g)", n=TILES)
+    var_rows = out_2.rearrange("b (c n) i j t e g -> (b c) n (i j t e g)", n=TILES)
 
     with ExitStack() as ctx:
-        const = ctx.enter_context(tc.tile_pool(name="const", bufs=1))
-        grp_pool = ctx.enter_context(tc.tile_pool(name="grp", bufs=RING["grp"]))
-        xq_pool = ctx.enter_context(tc.tile_pool(name="xq", bufs=RING["xq"]))
-        y1m_pool = ctx.enter_context(tc.tile_pool(name="y1m", bufs=RING["y1m"]))
-        y1v_pool = ctx.enter_context(tc.tile_pool(name="y1v", bufs=RING["y1v"]))
-        da_pool = ctx.enter_context(tc.tile_pool(name="da", bufs=RING["da"]))
-        out_pool = ctx.enter_context(tc.tile_pool(name="outp", bufs=RING["out"]))
-        sum_pool = ctx.enter_context(tc.tile_pool(name="sump", bufs=RING["sum"]))
+        keep = ctx.enter_context(tc.tile_pool(name="keep", bufs=1))
+        grouped_pool = ctx.enter_context(tc.tile_pool(name="grouped", bufs=2))
+        xq_pool = ctx.enter_context(tc.tile_pool(name="xq", bufs=3))
+        ym_pool = ctx.enter_context(tc.tile_pool(name="ym", bufs=2))
+        yv_pool = ctx.enter_context(tc.tile_pool(name="yv", bufs=UNITS))
+        da_pool = ctx.enter_context(tc.tile_pool(name="da", bufs=3))
+        out_pool = ctx.enter_context(tc.tile_pool(name="outs", bufs=3))
+        sum_pool = ctx.enter_context(tc.tile_pool(name="sums", bufs=2))
         psum = ctx.enter_context(tc.psum_pool(name="psum", bufs=4))
         ctx.enter_context(tc.manual_schedule())
 
-        def rows(s):
-            return slice(first[s], first[s] + SIZES[s])
+        def tiles_of(s):
+            return slice(s * UNIT, (s + 1) * UNIT)
 
-        x_sb = const.tile([P, NT, K], BF16, name="x_sb")
-        wraw = const.tile([P, 4, 2 * NC], BF16, name="wraw")
-        bz = const.tile([P, P], BF16, name="bz")
-        smu = const.tile([P, NT * 16], BF16, name="smu")
-        svar = const.tile([P, NT * 16], BF16, name="svar")
-        sw = const.tile([P, NT * 8], BF16, name="sw")
-        nc.vector.memset(bz[:], 0.0)
-        nc.scalar.dma_start(out=svar[:], in_=svar_v)
-        nc.sync.dma_start(out=x_sb[:, rows(0), :], in_=xv[:, rows(0), :])
-        nc.scalar.dma_start(out=smu[:], in_=smu_v)
-        for u in range(2):
-            for w, off in ((tcm_w, 0), (tcv_w, NC)):
+        x_sb = keep.tile([P, TILES, K], BF16, name="x_sb")
+        w_raw = keep.tile([P, 4, 2 * NC], BF16, name="w_raw")
+        bias_rows = keep.tile([P, P], BF16, name="bias_rows")
+        smu = keep.tile([P, TILES * 16], BF16, name="smu")
+        svar = keep.tile([P, TILES * 16], BF16, name="svar")
+        sw = keep.tile([P, TILES * 8], BF16, name="sw")
+        nc.vector.memset(bias_rows[:], 0.0)
+        for w, first_column in ((tcm_w, 0), (tcv_w, NC)):
+            for u in range(2):
                 nc.sync.dma_start(
-                    out=wraw[:, 2 * u : 2 * u + 2, off : off + NC],
+                    out=w_raw[:, 2 * u : 2 * u + 2, first_column : first_column + NC],
                     in_=w[256 * u : 256 * u + 256, :].rearrange("(q e) c -> q e c", e=2),
                 )
-        nc.scalar.dma_start(out=sw[:], in_=sw_v)
-        nc.scalar.dma_start(out=bz[0:2, :], in_=tcm_b.rearrange("(r c) -> r c", r=2))
-        nc.scalar.dma_start(out=bz[2:4, :], in_=tcv_b.rearrange("(r c) -> r c", r=2))
-        for s in range(1, units):
-            nc.sync.dma_start(out=x_sb[:, rows(s), :], in_=xv[:, rows(s), :])
+        nc.scalar.dma_start(
+            out=svar[:], in_=s_var.rearrange("b (c n) j e g -> (b c) (n j e g)", n=TILES)
+        )
+        nc.scalar.dma_start(out=x_sb[:, 0 : UNIT // 2, :], in_=x_rows[:, 0 : UNIT // 2, :])
+        nc.scalar.dma_start(out=x_sb[:, UNIT // 2 : UNIT, :], in_=x_rows[:, UNIT // 2 : UNIT, :])
+        nc.scalar.dma_start(out=bias_rows[0:2, :], in_=tcm_b.rearrange("(r c) -> r c", r=2))
+        nc.scalar.dma_start(out=bias_rows[2:4, :], in_=tcv_b.rearrange("(r c) -> r c", r=2))
+        nc.scalar.dma_start(
+            out=smu[:], in_=s_mu.rearrange("b (c n) j e g -> (b c) (n j e g)", n=TILES)
+        )
+        nc.sync.dma_start(out=x_sb[:, tiles_of(1), :], in_=x_rows[:, tiles_of(1), :])
+        nc.scalar.dma_start(
+            out=sw[:], in_=s_weight.rearrange("b (c n) j e -> (b c) (n j e)", n=TILES)
+        )
+        for s in range(2, UNITS):
+            nc.sync.dma_start(out=x_sb[:, tiles_of(s), :], in_=x_rows[:, tiles_of(s), :])
 
-        ident = const.tile([P, P], F32, name="ident")
+        ident = keep.tile([P, P], F32, name="ident")
         masks.make_identity(nc, ident[:])
-        minus = const.tile([P, 1], F32, name="minus")
-        nc.vector.memset(minus[:], -1.0)
-        wgrp = const.tile([P, 2 * NC, 4], BF16, name="wgrp", align_bytes=64)
-        wq = const.tile([P, 2 * NC], U32, name="wq", align_bytes=64)
-        wsc = const.tile([P, 2 * NC], U8, name="wsc", align_bytes=64)
-        bf = const.tile([P, P], F32, name="bf")
-        b1 = const.tile([P, 4], F32, name="b1")
-        dnu = const.tile([P, NT, 2 * NC], F32, name="dnu")
-        m1e = const.tile([P, NT, 32], F32, name="m1e")
-        m1p = const.tile([P, NT, 32], F32, name="m1p")
-        v1p = const.tile([P, NT, 32], F32, name="v1p")
-        hae = const.tile([P, NT, 32], F32, name="hae")
-        vs = const.tile([P, NT * 8], F32, name="vs")
-        k0 = const.tile([P, NT * 8], F32, name="k0")
-        ke = const.tile([P, NT, 16], F32, name="ke")
+        minus_one = keep.tile([P, 1], F32, name="minus_one")
+        nc.vector.memset(minus_one[:], -1.0)
+        w_grouped = keep.tile([P, 2 * NC, 4], BF16, name="w_grouped", align_bytes=64)
+        w_codes = keep.tile([P, 2 * NC], U32, name="w_codes", align_bytes=64)
+        w_scales = keep.tile([P, 2 * NC], U8, name="w_scales", align_bytes=64)
+        bias_f32 = keep.tile([P, P], F32, name="bias_f32")
+        bias_plus_1 = keep.tile([P, BLOCKS], F32, name="bias_plus_1")
+        work = keep.tile([P, TILES, 2 * NC], F32, name="work")
+        m1 = keep.tile([P, TILES, JTG], F32, name="m1")
+        m1_plus_1 = keep.tile([P, TILES, JTG], F32, name="m1_plus_1")
+        v1_plus_1 = keep.tile([P, TILES, JTG], F32, name="v1_plus_1")
+        half_inv_a = keep.tile([P, TILES, JTG], F32, name="half_inv_a")
+        v1_sum = keep.tile([P, TILES * 8], F32, name="v1_sum")
+        offset_j = keep.tile([P, TILES * 8], F32, name="offset_j")
+        offset = keep.tile([P, TILES, JT], F32, name="offset")
 
-        live = {}
-        done = set()
+        alive = {}
 
-        def spread(small):
+        def repeat_t(small):
             return (
                 small[:]
                 .rearrange("p (a g) -> p a g", g=2)
                 .unsqueeze(2)
-                .to_broadcast([P, NT * 8, 2, 2])
+                .to_broadcast([P, TILES * 8, 2, 2])
             )
 
         def as_njtg(full):
             return full[:].rearrange("p n (j t g) -> p (n j) t g", t=2, g=2)
 
-        def prepare_state():
-            nc.scalar.activation(out=as_njtg(hae), in_=spread(svar), func=ACT.Exp, scale=-2.0)
-            nc.vector.tensor_scalar_add(out=as_njtg(v1p), in0=spread(svar), scalar1=1.0)
-            nc.vector.tensor_copy(out=as_njtg(m1e), in_=spread(smu))
-            nc.vector.tensor_scalar_add(out=m1p[:], in0=m1e[:], scalar1=1.0)
-            nc.vector.tensor_copy(out=bf[:], in_=bz[:])
-            nc.vector.tensor_scalar_mul(out=hae[:], in0=hae[:], scalar1=0.5)
+        def by_i(ap):
+            return ap.rearrange("p (i c) -> p i c", i=NI)
 
-        def prepare_rest():
+        def by_tile_and_i(ap):
+            return ap.rearrange("p n (i c) -> p n i c", i=NI)
+
+        def repeat_i(small, n, count):
+            width = small.shape[2]
+            return small[:, n : n + count, :].unsqueeze(2).to_broadcast([P, count, NI, width])
+
+        def halves(s):
+            return [(lo, s * UNIT + lo, UNIT // 2) for lo in range(0, UNIT, UNIT // 2)]
+
+        def quantise_weights():
+            for first_column in (0, NC):
+                columns = slice(first_column, first_column + NC)
+                nc.vector.tensor_copy(
+                    out=w_grouped[:, columns, :],
+                    in_=w_raw[:, :, columns].rearrange("p t c -> p c t"),
+                )
+            for first_column in (0, NC):
+                columns = slice(first_column, first_column + NC)
+                nc.vector.quantize_mx(
+                    out=w_codes[:, columns].bitcast(FP8X4),
+                    scales=w_scales[:, columns],
+                    in_=w_grouped[:, columns, :].rearrange("p c t -> p (c t)"),
+                )
+
+        def bias_to_partitions():
+            nc.vector.tensor_copy(out=bias_f32[:], in_=bias_rows[:])
+            turned = psum.tile([P, 512], F32, name="turned", tag="to_scalar")
+            nc.tensor.transpose(turned[:, 0:P], bias_f32[:], ident[:])
+            nc.vector.tensor_scalar_add(
+                out=bias_plus_1[:], in0=turned[:, 0:BLOCKS], scalar1=1.0
+            )
+
+        def spread_state():
+            nc.vector.tensor_scalar_add(out=as_njtg(v1_plus_1), in0=repeat_t(svar), scalar1=1.0)
+            nc.vector.tensor_copy(out=as_njtg(m1), in_=repeat_t(smu))
+            nc.vector.tensor_scalar_add(out=m1_plus_1[:], in0=m1[:], scalar1=1.0)
+            nc.vector.tensor_scalar_mul(out=half_inv_a[:], in0=half_inv_a[:], scalar1=0.5)
+
+        def scale_offset():
             pairs = svar[:].rearrange("p (a g) -> p a g", g=2)
-            nc.vector.tensor_tensor(out=vs[:], in0=pairs[:, :, 0], in1=pairs[:, :, 1], op=ALU.add)
+            nc.vector.tensor_tensor(
+                out=v1_sum[:], in0=pairs[:, :, 0], in1=pairs[:, :, 1], op=ALU.add
+            )
             nc.vector.scalar_tensor_tensor(
-                out=k0[:], in0=sw[:], scalar=2.0 - math.log(2.0 * math.pi), in1=vs[:],
+                out=offset_j[:], in0=sw[:], scalar=2.0 - math.log(2.0 * math.pi), in1=v1_sum[:],
                 op0=ALU.add, op1=ALU.subtract,
             )
             nc.vector.tensor_copy(
-                out=ke[:].rearrange("p n (j t) -> p (n j) t", t=2),
-                in_=k0[:].unsqueeze(2).to_broadcast([P, NT * 8, 2]),
+                out=offset[:].rearrange("p n (j t) -> p (n j) t", t=2),
+                in_=offset_j[:].unsqueeze(2).to_broadcast([P, TILES * 8, 2]),
             )
 
-        def prepare_weights():
-            nc.vector.tensor_copy(out=wgrp[:], in_=wraw[:].rearrange("p t c -> p c t"))
-            nc.vector.quantize_mx(
-                out=wq[:].bitcast(FP8X4), scales=wsc[:], in_=wgrp[:].rearrange("p c t -> p (c t)")
-            )
-
-        def bias_columns():
-            bt = psum.tile([P, 512], F32, name="bt", tag="pa")
-            nc.tensor.transpose(bt[:, 0:P], bf[:], ident[:])
-            nc.vector.tensor_scalar_add(out=b1[:], in0=bt[:, 0:4], scalar1=1.0)
-
-        def x_transpose(s):
-            done.add(("xt", s))
-            size = SIZES[s]
-            grp = grp_pool.tile([P, 4 * P * big], BF16, name="grp", align_bytes=64)
-            live[("grp", s)] = grp
-            for lo in range(0, size, 2):
-                cnt = min(2, size - lo)
-                xt = psum.tile([P, 2, 2 * P], F32, name="xt", tag="pa")
-                for j in range(cnt):
-                    words = x_sb[:, first[s] + lo + j, :].bitcast(F32)
+        def transpose_x(s):
+            grouped = grouped_pool.tile([P, 4 * ROWS], BF16, name="grouped", align_bytes=64)
+            alive[("grouped", s)] = grouped
+            for lo in range(0, UNIT, 2):
+                turned = psum.tile([P, 2, 2 * P], F32, name="x_turned", tag="to_scalar")
+                for j in range(2):
+                    words = x_sb[:, s * UNIT + lo + j, :].bitcast(F32)
                     for u in range(2):
                         nc.tensor.transpose(
-                            xt[:, u, j * P : (j + 1) * P], words[:, u * P : (u + 1) * P], ident[:]
+                            turned[:, u, j * P : (j + 1) * P],
+                            words[:, u * P : (u + 1) * P],
+                            ident[:],
                         )
                 nc.scalar.copy(
-                    out=grp[:].bitcast(F32)[:, lo * 2 * P : (lo + cnt) * 2 * P].rearrange(
+                    out=grouped[:].bitcast(F32)[:, lo * 2 * P : (lo + 2) * 2 * P].rearrange(
                         "p (r u) -> p r u", u=2
                     ),
-                    in_=xt[:, :, 0 : cnt * P].rearrange("p u r -> p r u"),
+                    in_=turned[:].rearrange("p u r -> p r u"),
                 )
 
-        def x_quantise(s):
-            assert ("xt", s) in done
-            done.add(("q", s))
-            wide = P * SIZES[s]
-            xq = xq_pool.tile([P, P * big], U32, name="xq", align_bytes=64)
-            xs = xq_pool.tile([P, P * big], U8, name="xs", align_bytes=64)
-            live[("xq", s)] = (xq, xs)
+        def quantise_x(s):
+            codes = xq_pool.tile([P, ROWS], U32, name="x_codes", align_bytes=64)
+            scales = xq_pool.tile([P, ROWS], U8, name="x_scales", align_bytes=64)
+            alive[("xq", s)] = (codes, scales)
             nc.vector.quantize_mx(
-                out=xq[:, 0:wide].bitcast(FP8X4), scales=xs[:, 0:wide],
-                in_=live[("grp", s)][:, 0 : 4 * wide],
+                out=codes[:].bitcast(FP8X4), scales=scales[:], in_=alive[("grouped", s)][:]
             )
 
         def project(s):
-            assert ("q", s) in done
-            done.add(("mm", s))
-            wide = P * SIZES[s]
-            xq, xs = live[("xq", s)]
-            y1 = (
-                y1m_pool.tile([P, 2, P * big], F32, name="y1m"),
-                y1v_pool.tile([P, 2, P * big], F32, name="y1v"),
+            codes, scales = alive[("xq", s)]
+            y = (
+                ym_pool.tile([P, 2, ROWS], F32, name="ym"),
+                yv_pool.tile([P, 2, ROWS], F32, name="yv"),
             )
-            live[("y1", s)] = y1
-            for cb in range(4):
-                pc = psum.tile([P, 512], F32, name="pc", tag="pa")
+            alive[("y", s)] = y
+            for block in range(BLOCKS):
+                columns = slice(block * P, (block + 1) * P)
+                product = psum.tile([P, ROWS], F32, name="product", tag="to_scalar")
                 nc.tensor.matmul_mx(
-                    out=pc[:, 0:wide],
-                    lhsT=wq[:, cb * P : (cb + 1) * P].bitcast(FP8X4),
-                    lhsT_scale=wsc[:, cb * P : (cb + 1) * P],
-                    rhs=xq[:, 0:wide].bitcast(FP8X4),
-                    rhs_scale=xs[:, 0:wide],
+                    out=product[:],
+                    lhsT=w_codes[:, columns].bitcast(FP8X4),
+                    lhsT_scale=w_scales[:, columns],
+                    rhs=codes[:].bitcast(FP8X4),
+                    rhs_scale=scales[:],
                     start=True,
                     stop=True,
                 )
                 nc.scalar.activation(
-                    out=y1[cb // 2][:, cb % 2, 0:wide], in_=pc[:, 0:wide], func=ACT.Relu,
-                    bias=b1[:, cb : cb + 1], scale=1.0,
+                    out=y[block // 2][:, block % 2, :], in_=product[:], func=ACT.Relu,
+                    bias=bias_plus_1[:, block : block + 1], scale=1.0,
                 )
 
-        def by_i(ap):
-            return ap.rearrange("p (i c) -> p i c", i=8)
-
-        def back_transpose(s):
-            assert ("mm", s) in done
-            done.add(("bt", s))
-            y1 = live[("y1", s)]
-            if POOL_DA:
-                live[("da", s)] = da_pool.tile([P, big, NC], F32, name="da")
+        def back_to_rows(s):
+            y = alive[("y", s)]
+            da = da_pool.tile([P, UNIT, NC], F32, name="da")
+            alive[("da", s)] = da
             banks = []
 
-            def clip_and_subtract(tl, half, small):
-                n = first[s] + tl
+            def clip_and_subtract(lo, half, state_plus_1):
+                n = s * UNIT + lo
+                columns = slice(half * NC, (half + 1) * NC)
                 nc.vector.scalar_tensor_tensor(
-                    out=by_i(dnu[:, n, half * NC : (half + 1) * NC]),
-                    in0=by_i(banks[tl][:, half * NC : (half + 1) * NC]),
+                    out=by_i(work[:, n, columns]),
+                    in0=by_i(banks[lo][:, columns]),
                     scalar=2.0,
-                    in1=small[:, n, :].unsqueeze(1).to_broadcast([P, 8, 32]),
+                    in1=state_plus_1[:, n, :].unsqueeze(1).to_broadcast([P, NI, JTG]),
                     op0=ALU.min,
                     op1=ALU.subtract,
                 )
 
-            for tl in range(SIZES[s]):
-                n = first[s] + tl
-                yt = psum.tile([P, 512], F32, name="yt", tag="pv")
-                banks.append(yt)
-                for cb in range(4):
+            for lo in range(UNIT):
+                n = s * UNIT + lo
+                bank = psum.tile([P, 2 * NC], F32, name="y_rows", tag="to_vector")
+                banks.append(bank)
+                for block in range(BLOCKS):
                     nc.tensor.transpose(
-                        yt[:, cb * P : (cb + 1) * P],
-                        y1[cb // 2][:, cb % 2, tl * P : (tl + 1) * P],
+                        bank[:, block * P : (block + 1) * P],
+                        y[block // 2][:, block % 2, lo * P : (lo + 1) * P],
                         ident[:],
                     )
-                clip_and_subtract(tl, 0, m1p)
-                if not MFIRST:
-                    clip_and_subtract(tl, 1, v1p)
-                if POOL_DA:
-                    nc.gpsimd.tensor_tensor(
-                        out=by_i(live[("da", s)][:, tl, :]),
-                        in0=by_i(dnu[:, n, 0:NC]),
-                        in1=hae[:, n, :].unsqueeze(1).to_broadcast([P, 8, 32]),
-                        op=ALU.mult,
-                    )
-            if MFIRST:
-                for tl in range(SIZES[s]):
-                    clip_and_subtract(tl, 1, v1p)
-
-        def pieces(s):
-            step = max(1, SIZES[s] // SPLIT)
-            return [(lo, min(step, SIZES[s] - lo)) for lo in range(0, SIZES[s], step)]
-
-        def over_i(small, n, cnt, width):
-            return small[:, n : n + cnt, :].unsqueeze(2).to_broadcast([P, cnt, 8, width])
-
-        def split_i(ap):
-            return ap.rearrange("p n (i c) -> p n i c", i=8)
+                clip_and_subtract(lo, 0, m1_plus_1)
+                nc.gpsimd.tensor_tensor(
+                    out=by_i(da[:, lo, :]),
+                    in0=by_i(work[:, n, 0:NC]),
+                    in1=half_inv_a[:, n, :].unsqueeze(1).to_broadcast([P, NI, JTG]),
+                    op=ALU.mult,
+                )
+            for lo in range(UNIT):
+                clip_and_subtract(lo, 1, v1_plus_1)
 
         def sigmoid(s):
-            assert ("bt", s) in done
-            done.add(("sg", s))
-            u = dnu[:, rows(s), NC : 2 * NC]
+            u = work[:, tiles_of(s), NC : 2 * NC]
             nc.scalar.activation(out=u, in_=u, func=ACT.Sigmoid, scale=-2.0)
 
-        def gain(s):
-            assert ("sg", s) in done
-            done.add(("g", s))
-            g = out_pool.tile([P, big, NC], F32, name="gmu")
-            live[("g", s)] = g
-            for lo, cnt in pieces(s):
-                n = first[s] + lo
-                nc.vector.tensor_tensor(
-                    out=g[:, lo : lo + cnt, :], in0=dnu[:, n : n + cnt, 0:NC],
-                    in1=dnu[:, n : n + cnt, NC : 2 * NC], op=ALU.mult,
-                )
+        def front(s):
+            if 0 <= s < UNITS:
+                back_to_rows(s)
+            if 0 <= s + AHEAD_QUANTISE < UNITS:
+                quantise_x(s + AHEAD_QUANTISE)
+            if s == 0:
+                scale_offset()
+            if 0 <= s + AHEAD_PROJECT < UNITS:
+                project(s + AHEAD_PROJECT)
+            if 0 <= s + AHEAD_TRANSPOSE < UNITS:
+                transpose_x(s + AHEAD_TRANSPOSE)
+                if s + AHEAD_TRANSPOSE == 0:
+                    bias_to_partitions()
+            if 0 <= s < UNITS:
+                sigmoid(s)
 
-        def mean(s):
-            assert ("g", s) in done
-            done.add(("ms", s))
-            g = live[("g", s)]
-            if not POOL_DA:
-                live[("da", s)] = da_pool.tile([P, big, NC], F32, name="da")
-                for lo, cnt in pieces(s):
-                    n = first[s] + lo
-                    nc.vector.tensor_tensor(
-                        out=split_i(live[("da", s)][:, lo : lo + cnt, :]),
-                        in0=split_i(dnu[:, n : n + cnt, 0:NC]),
-                        in1=over_i(hae, n, cnt, 32), op=ALU.mult,
-                    )
-            for lo, cnt in pieces(s):
-                n = first[s] + lo
+        def products(s):
+            g = out_pool.tile([P, UNIT, NC], F32, name="g")
+            da = alive[("da", s)]
+            for lo, n, count in halves(s):
                 nc.vector.tensor_tensor(
-                    out=dnu[:, n : n + cnt, 0:NC], in0=g[:, lo : lo + cnt, :],
-                    in1=live[("da", s)][:, lo : lo + cnt, :], op=ALU.mult,
+                    out=g[:, lo : lo + count, :], in0=work[:, n : n + count, 0:NC],
+                    in1=work[:, n : n + count, NC : 2 * NC], op=ALU.mult,
                 )
-            for lo, cnt in pieces(s):
-                n = first[s] + lo
+            for lo, n, count in halves(s):
                 nc.vector.tensor_tensor(
-                    out=split_i(g[:, lo : lo + cnt, :]), in0=split_i(g[:, lo : lo + cnt, :]),
-                    in1=over_i(m1e, n, cnt, 32), op=ALU.add,
+                    out=work[:, n : n + count, 0:NC], in0=g[:, lo : lo + count, :],
+                    in1=da[:, lo : lo + count, :], op=ALU.mult,
                 )
-            nc.sync.dma_start(out=mu_v[:, rows(s), :], in_=g[:, 0 : SIZES[s], :])
+            for lo, n, count in halves(s):
+                nc.vector.tensor_tensor(
+                    out=by_tile_and_i(g[:, lo : lo + count, :]),
+                    in0=by_tile_and_i(g[:, lo : lo + count, :]),
+                    in1=repeat_i(m1, n, count), op=ALU.add,
+                )
+            nc.sync.dma_start(out=mu_rows[:, tiles_of(s), :], in_=g[:])
 
         def log_weight(s):
-            assert ("g", s) in done
-            done.add(("ln", s))
-            wc = dnu[:, rows(s), NC : 2 * NC]
+            wc = work[:, tiles_of(s), NC : 2 * NC]
             nc.scalar.activation(out=wc, in_=wc, func=ACT.Ln)
-            if POOL_HL:
-                for lo in range(first[s], first[s] + SIZES[s]):
-                    part = dnu[:, lo : lo + 1, NC : 2 * NC]
-                    nc.gpsimd.tensor_scalar(
-                        out=part, in0=part, scalar1=0.5, scalar2=-1.0, op0=ALU.mult, op1=ALU.add
-                    )
-            else:
-                nc.scalar.activation(out=wc, in_=wc, func=ACT.Identity, bias=minus[:], scale=0.5)
+
+        def half_log(s):
+            log_wc = work[:, tiles_of(s), NC : 2 * NC]
+            nc.scalar.activation(
+                out=log_wc, in_=log_wc, func=ACT.Identity, bias=minus_one[:], scale=0.5
+            )
 
         def variance(s):
-            assert ("ln", s) in done
-            done.add(("va", s))
-            size = SIZES[s]
-            vt = out_pool.tile([P, big, NC], F32, name="var")
-            y1 = live[("y1", s)]
-            for lo in range(0, size, 2):
-                cnt = min(2, size - lo)
-                yv = psum.tile([P, 2, NC], F32, name="yv", tag="pv")
-                for j in range(cnt):
-                    tl = lo + j
-                    for cb in range(2):
+            var = out_pool.tile([P, UNIT, NC], F32, name="var")
+            yv = alive[("y", s)][1]
+            for lo, n, count in halves(s):
+                bank = psum.tile([P, 2, NC], F32, name="yv_rows", tag="to_vector")
+                for j in range(count):
+                    for block in range(2):
                         nc.tensor.transpose(
-                            yv[:, j, cb * P : (cb + 1) * P],
-                            y1[1][:, cb, tl * P : (tl + 1) * P],
+                            bank[:, j, block * P : (block + 1) * P],
+                            yv[:, block, (lo + j) * P : (lo + j + 1) * P],
                             ident[:],
                         )
-                n = first[s] + lo
                 nc.vector.scalar_tensor_tensor(
-                    out=vt[:, lo : lo + cnt, :],
-                    in0=yv[:, 0:cnt, :],
+                    out=var[:, lo : lo + count, :],
+                    in0=bank[:],
                     scalar=2.0,
-                    in1=dnu[:, n : n + cnt, NC : 2 * NC],
+                    in1=work[:, n : n + count, NC : 2 * NC],
                     op0=ALU.min,
                     op1=ALU.add,
                 )
-            nc.sync.dma_start(out=var_v[:, rows(s), :], in_=vt[:, 0:size, :])
+            nc.sync.dma_start(out=var_rows[:, tiles_of(s), :], in_=var[:])
 
-        def half_terms(s):
-            assert ("ln", s) in done and ("ms", s) in done
-            done.add(("lq", s))
-            for lo, cnt in pieces(s):
-                n = first[s] + lo
+        def summands(s):
+            for lo, n, count in halves(s):
                 nc.vector.tensor_tensor(
-                    out=dnu[:, n : n + cnt, 0:NC], in0=dnu[:, n : n + cnt, NC : 2 * NC],
-                    in1=dnu[:, n : n + cnt, 0:NC], op=ALU.subtract,
+                    out=work[:, n : n + count, 0:NC], in0=work[:, n : n + count, NC : 2 * NC],
+                    in1=work[:, n : n + count, 0:NC], op=ALU.subtract,
                 )
 
-        def pair_sum(s):
-            eng = nc.gpsimd if POOL_P1 and s != units - 1 else nc.vector
-            ps = sum_pool.tile([P, big, P], F32, name="ps")
-            live[("ps", s)] = ps
-            for lo, cnt in pieces(s):
-                n = first[s] + lo
-                pair = dnu[:, n : n + cnt, 0:NC].rearrange("p n (c g) -> p n c g", g=2)
-                eng.tensor_tensor(
-                    out=ps[:, lo : lo + cnt, :], in0=pair[:, :, :, 0], in1=pair[:, :, :, 1],
+        def sum_over_g(s):
+            engine = nc.gpsimd if s + 1 < UNITS else nc.vector
+            sums = sum_pool.tile([P, UNIT, NC // 2], F32, name="sums")
+            alive[("sums", s)] = sums
+            for lo, n, count in halves(s):
+                pair = work[:, n : n + count, 0:NC].rearrange("p n (c g) -> p n c g", g=2)
+                engine.tensor_tensor(
+                    out=sums[:, lo : lo + count, :], in0=pair[:, :, :, 0], in1=pair[:, :, :, 1],
                     op=ALU.add,
                 )
 
         def log_scale(s):
-            assert ("lq", s) in done
-            ps = live[("ps", s)]
-            sc = out_pool.tile([P, big, P], F32, name="sc")
-            for lo, cnt in pieces(s):
-                n = first[s] + lo
+            sums = alive[("sums", s)]
+            scale = out_pool.tile([P, UNIT, NC // 2], F32, name="scale")
+            for lo, n, count in halves(s):
                 nc.vector.tensor_tensor(
-                    out=split_i(sc[:, lo : lo + cnt, :]), in0=split_i(ps[:, lo : lo + cnt, :]),
-                    in1=over_i(ke, n, cnt, 16), op=ALU.add,
+                    out=by_tile_and_i(scale[:, lo : lo + count, :]),
+                    in0=by_tile_and_i(sums[:, lo : lo + count, :]),
+                    in1=repeat_i(offset, n, count), op=ALU.add,
                 )
-            nc.sync.dma_start(out=sc_v[:, rows(s), :], in_=sc[:, 0 : SIZES[s], :])
-
-        period_of = {}
-        for index, period in enumerate(PERIODS):
-            for s in period:
-                period_of[s] = index
-        issued = {"sg": set(), "ln": set()}
-        held = {"sg": [], "ln": []}
-
-        def may_run(kind, s):
-            index = period_of[s]
-            if kind == "sg":
-                return index == 0 or all(v in issued["ln"] for v in PERIODS[index - 1])
-            return all(v in issued["sg"] for v in PERIODS[index])
-
-        def table_work(kind, s):
-            held[kind] = held[kind] + [s]
-            moved = True
-            while moved:
-                moved = False
-                for k2, work in (("sg", sigmoid), ("ln", log_weight)):
-                    for v in held[k2]:
-                        if may_run(k2, v):
-                            work(v)
-                            issued[k2].add(v)
-                            moved = True
-                    held[k2] = [v for v in held[k2] if v not in issued[k2]]
-
-        def front(s):
-            if 0 <= s < units:
-                back_transpose(s)
-            if 0 <= s + QL < units:
-                x_quantise(s + QL)
-            if s == 0:
-                prepare_rest()
-            if 0 <= s + ML < units:
-                project(s + ML)
-            if 0 <= s + XL < units:
-                x_transpose(s + XL)
-                if s + XL == 0:
-                    bias_columns()
-            if 0 <= s < units:
-                table_work("sg", s)
-
-        def products(s):
-            gain(s)
-            table_work("ln", s)
-            mean(s)
+            nc.sync.dma_start(out=scale_rows[:, tiles_of(s), :], in_=scale[:])
 
         def logs(s):
-            if not PIPE_ES:
+            if s == 0:
                 variance(s)
-                half_terms(s)
-                pair_sum(s)
-                log_scale(s)
-                return
-            period = PERIODS[period_of[s]]
-            if s == period[0]:
-                variance(s)
-            half_terms(s)
-            pair_sum(s)
-            if s != period[-1]:
+            summands(s)
+            sum_over_g(s)
+            if s + 1 < UNITS:
                 variance(s + 1)
             log_scale(s)
 
-        jobs = []
-        for period in PERIODS:
-            jobs.extend([(products, s) for s in period])
-            jobs.extend([(logs, s) for s in period])
-        prepare_state()
-        prepare_weights()
-        for s in range(-XL, LEAD):
+        nc.scalar.activation(
+            out=as_njtg(half_inv_a), in_=repeat_t(svar), func=ACT.Exp, scale=-2.0
+        )
+        quantise_weights()
+        for s in range(-AHEAD_TRANSPOSE, AHEAD_FRONT):
             front(s)
-        for index, job in enumerate(jobs):
-            job[0](job[1])
-            if index + LEAD < units:
-                front(index + LEAD)
+            if s == -AHEAD_QUANTISE:
+                spread_state()
+        jobs = [(products, s) for s in range(UNITS)] + [(logs, s) for s in range(UNITS)]
+        for index, (job, s) in enumerate(jobs):
+            ahead = index + AHEAD_LN - UNITS
+            if 0 <= ahead < UNITS:
+                log_weight(ahead)
+            if 0 <= ahead - 1 < UNITS:
+                half_log(ahead - 1)
+            job(s)
+            if index + AHEAD_FRONT < UNITS:
+                front(index + AHEAD_FRONT)

import math
from contextlib import ExitStack

import concourse.masks as masks
import concourse.mybir as mybir

F32 = mybir.dt.float32
BF16 = mybir.dt.bfloat16
U32 = mybir.dt.uint32
U8 = mybir.dt.uint8
FP8X4 = mybir.dt.float8_e4m3fn_x4
ALU = mybir.AluOpType
ACT = mybir.ActivationFunctionType

FLOPS = 2 * 4096 * 512 * 512

P = 128
TILES = 32
UNIT = 4
UNITS = TILES // UNIT
ROWS = UNIT * P
K = 512
NC = 256
NI = 8
JTG = NC // NI
JT = JTG // 2
BLOCKS = 2 * NC // P
AHEAD_PROJECT = 1
AHEAD_QUANTISE = 2
AHEAD_TRANSPOSE = 3
AHEAD_FRONT = 2
AHEAD_LN = 2


def tile_chainlveg_pa_t_kernel(
    tc, x, s_weight, s_mu, s_var, tcm_w, tcm_b, tcv_w, tcv_b, out_0, out_1, out_2
):
    nc = tc.nc
    x_rows = x.rearrange("b (c n) k -> (b c) n k", n=TILES)
    scale_rows = out_0.rearrange("b (c n) i j t e -> (b c) n (i j t e)", n=TILES)
    mu_rows = out_1.rearrange("b (c n) i j t e g -> (b c) n (i j t e g)", n=TILES)
    var_rows = out_2.rearrange("b (c n) i j t e g -> (b c) n (i j t e g)", n=TILES)

    with ExitStack() as ctx:
        keep = ctx.enter_context(tc.tile_pool(name="keep", bufs=1))
        grouped_pool = ctx.enter_context(tc.tile_pool(name="grouped", bufs=2))
        xq_pool = ctx.enter_context(tc.tile_pool(name="xq", bufs=3))
        ym_pool = ctx.enter_context(tc.tile_pool(name="ym", bufs=2))
        yv_pool = ctx.enter_context(tc.tile_pool(name="yv", bufs=UNITS))
        da_pool = ctx.enter_context(tc.tile_pool(name="da", bufs=3))
        out_pool = ctx.enter_context(tc.tile_pool(name="outs", bufs=3))
        sum_pool = ctx.enter_context(tc.tile_pool(name="sums", bufs=2))
        psum = ctx.enter_context(tc.psum_pool(name="psum", bufs=4))
        ctx.enter_context(tc.manual_schedule())

        def tiles_of(s):
            return slice(s * UNIT, (s + 1) * UNIT)

        x_sb = keep.tile([P, TILES, K], BF16, name="x_sb")
        w_raw = keep.tile([P, 4, 2 * NC], BF16, name="w_raw")
        bias_rows = keep.tile([P, P], BF16, name="bias_rows")
        smu = keep.tile([P, TILES * 16], BF16, name="smu")
        svar = keep.tile([P, TILES * 16], BF16, name="svar")
        sw = keep.tile([P, TILES * 8], BF16, name="sw")
        nc.vector.memset(bias_rows[:], 0.0)
        for w, first_column in ((tcm_w, 0), (tcv_w, NC)):
            for u in range(2):
                nc.sync.dma_start(
                    out=w_raw[:, 2 * u : 2 * u + 2, first_column : first_column + NC],
                    in_=w[256 * u : 256 * u + 256, :].rearrange("(q e) c -> q e c", e=2),
                )
        nc.scalar.dma_start(
            out=svar[:], in_=s_var.rearrange("b (c n) j e g -> (b c) (n j e g)", n=TILES)
        )
        nc.scalar.dma_start(out=x_sb[:, 0 : UNIT // 2, :], in_=x_rows[:, 0 : UNIT // 2, :])
        nc.scalar.dma_start(out=x_sb[:, UNIT // 2 : UNIT, :], in_=x_rows[:, UNIT // 2 : UNIT, :])
        nc.scalar.dma_start(out=bias_rows[0:2, :], in_=tcm_b.rearrange("(r c) -> r c", r=2))
        nc.scalar.dma_start(out=bias_rows[2:4, :], in_=tcv_b.rearrange("(r c) -> r c", r=2))
        nc.scalar.dma_start(
            out=smu[:], in_=s_mu.rearrange("b (c n) j e g -> (b c) (n j e g)", n=TILES)
        )
        nc.sync.dma_start(out=x_sb[:, tiles_of(1), :], in_=x_rows[:, tiles_of(1), :])
        nc.scalar.dma_start(
            out=sw[:], in_=s_weight.rearrange("b (c n) j e -> (b c) (n j e)", n=TILES)
        )
        for s in range(2, UNITS):
            nc.sync.dma_start(out=x_sb[:, tiles_of(s), :], in_=x_rows[:, tiles_of(s), :])

        ident = keep.tile([P, P], F32, name="ident")
        masks.make_identity(nc, ident[:])
        minus_one = keep.tile([P, 1], F32, name="minus_one")
        nc.vector.memset(minus_one[:], -1.0)
        w_grouped = keep.tile([P, 2 * NC, 4], BF16, name="w_grouped", align_bytes=64)
        w_codes = keep.tile([P, 2 * NC], U32, name="w_codes", align_bytes=64)
        w_scales = keep.tile([P, 2 * NC], U8, name="w_scales", align_bytes=64)
        bias_f32 = keep.tile([P, P], F32, name="bias_f32")
        bias_plus_1 = keep.tile([P, BLOCKS], F32, name="bias_plus_1")
        work = keep.tile([P, TILES, 2 * NC], F32, name="work")
        m1 = keep.tile([P, TILES, JTG], F32, name="m1")
        m1_plus_1 = keep.tile([P, TILES, JTG], F32, name="m1_plus_1")
        v1_plus_1 = keep.tile([P, TILES, JTG], F32, name="v1_plus_1")
        half_inv_a = keep.tile([P, TILES, JTG], F32, name="half_inv_a")
        v1_sum = keep.tile([P, TILES * 8], F32, name="v1_sum")
        offset_j = keep.tile([P, TILES * 8], F32, name="offset_j")
        offset = keep.tile([P, TILES, JT], F32, name="offset")

        alive = {}

        def repeat_t(small):
            return (
                small[:]
                .rearrange("p (a g) -> p a g", g=2)
                .unsqueeze(2)
                .to_broadcast([P, TILES * 8, 2, 2])
            )

        def as_njtg(full):
            return full[:].rearrange("p n (j t g) -> p (n j) t g", t=2, g=2)

        def by_i(ap):
            return ap.rearrange("p (i c) -> p i c", i=NI)

        def by_tile_and_i(ap):
            return ap.rearrange("p n (i c) -> p n i c", i=NI)

        def repeat_i(small, n, count):
            width = small.shape[2]
            return small[:, n : n + count, :].unsqueeze(2).to_broadcast([P, count, NI, width])

        def halves(s):
            return [(lo, s * UNIT + lo, UNIT // 2) for lo in range(0, UNIT, UNIT // 2)]

        def quantise_weights():
            for first_column in (0, NC):
                columns = slice(first_column, first_column + NC)
                nc.vector.tensor_copy(
                    out=w_grouped[:, columns, :],
                    in_=w_raw[:, :, columns].rearrange("p t c -> p c t"),
                )
            for first_column in (0, NC):
                columns = slice(first_column, first_column + NC)
                nc.vector.quantize_mx(
                    out=w_codes[:, columns].bitcast(FP8X4),
                    scales=w_scales[:, columns],
                    in_=w_grouped[:, columns, :].rearrange("p c t -> p (c t)"),
                )

        def bias_to_partitions():
            nc.vector.tensor_copy(out=bias_f32[:], in_=bias_rows[:])
            turned = psum.tile([P, 512], F32, name="turned", tag="to_scalar")
            nc.tensor.transpose(turned[:, 0:P], bias_f32[:], ident[:])
            nc.vector.tensor_scalar_add(
                out=bias_plus_1[:], in0=turned[:, 0:BLOCKS], scalar1=1.0
            )

        def spread_state():
            nc.vector.tensor_scalar_add(out=as_njtg(v1_plus_1), in0=repeat_t(svar), scalar1=1.0)
            nc.vector.tensor_copy(out=as_njtg(m1), in_=repeat_t(smu))
            nc.vector.tensor_scalar_add(out=m1_plus_1[:], in0=m1[:], scalar1=1.0)
            nc.vector.tensor_scalar_mul(out=half_inv_a[:], in0=half_inv_a[:], scalar1=0.5)

        def scale_offset():
            pairs = svar[:].rearrange("p (a g) -> p a g", g=2)
            nc.vector.tensor_tensor(
                out=v1_sum[:], in0=pairs[:, :, 0], in1=pairs[:, :, 1], op=ALU.add
            )
            nc.vector.scalar_tensor_tensor(
                out=offset_j[:], in0=sw[:], scalar=2.0 - math.log(2.0 * math.pi), in1=v1_sum[:],
                op0=ALU.add, op1=ALU.subtract,
            )
            nc.vector.tensor_copy(
                out=offset[:].rearrange("p n (j t) -> p (n j) t", t=2),
                in_=offset_j[:].unsqueeze(2).to_broadcast([P, TILES * 8, 2]),
            )

        def transpose_x(s):
            grouped = grouped_pool.tile([P, 4 * ROWS], BF16, name="grouped", align_bytes=64)
            alive[("grouped", s)] = grouped
            for lo in range(0, UNIT, 2):
                turned = psum.tile([P, 2, 2 * P], F32, name="x_turned", tag="to_scalar")
                for j in range(2):
                    words = x_sb[:, s * UNIT + lo + j, :].bitcast(F32)
                    for u in range(2):
                        nc.tensor.transpose(
                            turned[:, u, j * P : (j + 1) * P],
                            words[:, u * P : (u + 1) * P],
                            ident[:],
                        )
                nc.scalar.copy(
                    out=grouped[:].bitcast(F32)[:, lo * 2 * P : (lo + 2) * 2 * P].rearrange(
                        "p (r u) -> p r u", u=2
                    ),
                    in_=turned[:].rearrange("p u r -> p r u"),
                )

        def quantise_x(s):
            codes = xq_pool.tile([P, ROWS], U32, name="x_codes", align_bytes=64)
            scales = xq_pool.tile([P, ROWS], U8, name="x_scales", align_bytes=64)
            alive[("xq", s)] = (codes, scales)
            nc.vector.quantize_mx(
                out=codes[:].bitcast(FP8X4), scales=scales[:], in_=alive[("grouped", s)][:]
            )

        def project(s):
            codes, scales = alive[("xq", s)]
            y = (
                ym_pool.tile([P, 2, ROWS], F32, name="ym"),
                yv_pool.tile([P, 2, ROWS], F32, name="yv"),
            )
            alive[("y", s)] = y
            for block in range(BLOCKS):
                columns = slice(block * P, (block + 1) * P)
                product = psum.tile([P, ROWS], F32, name="product", tag="to_scalar")
                nc.tensor.matmul_mx(
                    out=product[:],
                    lhsT=w_codes[:, columns].bitcast(FP8X4),
                    lhsT_scale=w_scales[:, columns],
                    rhs=codes[:].bitcast(FP8X4),
                    rhs_scale=scales[:],
                    start=True,
                    stop=True,
                )
                nc.scalar.activation(
                    out=y[block // 2][:, block % 2, :], in_=product[:], func=ACT.Relu,
                    bias=bias_plus_1[:, block : block + 1], scale=1.0,
                )

        def back_to_rows(s):
            y = alive[("y", s)]
            da = da_pool.tile([P, UNIT, NC], F32, name="da")
            alive[("da", s)] = da
            banks = []

            def clip_and_subtract(lo, half, state_plus_1):
                n = s * UNIT + lo
                columns = slice(half * NC, (half + 1) * NC)
                nc.vector.scalar_tensor_tensor(
                    out=by_i(work[:, n, columns]),
                    in0=by_i(banks[lo][:, columns]),
                    scalar=2.0,
                    in1=state_plus_1[:, n, :].unsqueeze(1).to_broadcast([P, NI, JTG]),
                    op0=ALU.min,
                    op1=ALU.subtract,
                )

            for lo in range(UNIT):
                n = s * UNIT + lo
                bank = psum.tile([P, 2 * NC], F32, name="y_rows", tag="to_vector")
                banks.append(bank)
                for block in range(BLOCKS):
                    nc.tensor.transpose(
                        bank[:, block * P : (block + 1) * P],
                        y[block // 2][:, block % 2, lo * P : (lo + 1) * P],
                        ident[:],
                    )
                clip_and_subtract(lo, 0, m1_plus_1)
                nc.gpsimd.tensor_tensor(
                    out=by_i(da[:, lo, :]),
                    in0=by_i(work[:, n, 0:NC]),
                    in1=half_inv_a[:, n, :].unsqueeze(1).to_broadcast([P, NI, JTG]),
                    op=ALU.mult,
                )
            for lo in range(UNIT):
                clip_and_subtract(lo, 1, v1_plus_1)

        def sigmoid(s):
            u = work[:, tiles_of(s), NC : 2 * NC]
            nc.scalar.activation(out=u, in_=u, func=ACT.Sigmoid, scale=-2.0)

        def front(s):
            if 0 <= s < UNITS:
                back_to_rows(s)
            if 0 <= s + AHEAD_QUANTISE < UNITS:
                quantise_x(s + AHEAD_QUANTISE)
            if s == 0:
                scale_offset()
            if 0 <= s + AHEAD_PROJECT < UNITS:
                project(s + AHEAD_PROJECT)
            if 0 <= s + AHEAD_TRANSPOSE < UNITS:
                transpose_x(s + AHEAD_TRANSPOSE)
                if s + AHEAD_TRANSPOSE == 0:
                    bias_to_partitions()
            if 0 <= s < UNITS:
                sigmoid(s)

        def products(s):
            g = out_pool.tile([P, UNIT, NC], F32, name="g")
            da = alive[("da", s)]
            for lo, n, count in halves(s):
                nc.vector.tensor_tensor(
                    out=g[:, lo : lo + count, :], in0=work[:, n : n + count, 0:NC],
                    in1=work[:, n : n + count, NC : 2 * NC], op=ALU.mult,
                )
            for lo, n, count in halves(s):
                nc.vector.tensor_tensor(
                    out=work[:, n : n + count, 0:NC], in0=g[:, lo : lo + count, :],
                    in1=da[:, lo : lo + count, :], op=ALU.mult,
                )
            for lo, n, count in halves(s):
                nc.vector.tensor_tensor(
                    out=by_tile_and_i(g[:, lo : lo + count, :]),
                    in0=by_tile_and_i(g[:, lo : lo + count, :]),
                    in1=repeat_i(m1, n, count), op=ALU.add,
                )
            nc.sync.dma_start(out=mu_rows[:, tiles_of(s), :], in_=g[:])

        def log_weight(s):
            wc = work[:, tiles_of(s), NC : 2 * NC]
            nc.scalar.activation(out=wc, in_=wc, func=ACT.Ln)

        def half_log(s):
            log_wc = work[:, tiles_of(s), NC : 2 * NC]
            nc.scalar.activation(
                out=log_wc, in_=log_wc, func=ACT.Identity, bias=minus_one[:], scale=0.5
            )

        def variance(s):
            var = out_pool.tile([P, UNIT, NC], F32, name="var")
            yv = alive[("y", s)][1]
            for lo, n, count in halves(s):
                bank = psum.tile([P, 2, NC], F32, name="yv_rows", tag="to_vector")
                for j in range(count):
                    for block in range(2):
                        nc.tensor.transpose(
                            bank[:, j, block * P : (block + 1) * P],
                            yv[:, block, (lo + j) * P : (lo + j + 1) * P],
                            ident[:],
                        )
                nc.vector.scalar_tensor_tensor(
                    out=var[:, lo : lo + count, :],
                    in0=bank[:],
                    scalar=2.0,
                    in1=work[:, n : n + count, NC : 2 * NC],
                    op0=ALU.min,
                    op1=ALU.add,
                )
            nc.sync.dma_start(out=var_rows[:, tiles_of(s), :], in_=var[:])

        def summands(s):
            for lo, n, count in halves(s):
                nc.vector.tensor_tensor(
                    out=work[:, n : n + count, 0:NC], in0=work[:, n : n + count, NC : 2 * NC],
                    in1=work[:, n : n + count, 0:NC], op=ALU.subtract,
                )

        def sum_over_g(s):
            engine = nc.gpsimd if s + 1 < UNITS else nc.vector
            sums = sum_pool.tile([P, UNIT, NC // 2], F32, name="sums")
            alive[("sums", s)] = sums
            for lo, n, count in halves(s):
                pair = work[:, n : n + count, 0:NC].rearrange("p n (c g) -> p n c g", g=2)
                engine.tensor_tensor(
                    out=sums[:, lo : lo + count, :], in0=pair[:, :, :, 0], in1=pair[:, :, :, 1],
                    op=ALU.add,
                )

        def log_scale(s):
            sums = alive[("sums", s)]
            scale = out_pool.tile([P, UNIT, NC // 2], F32, name="scale")
            for lo, n, count in halves(s):
                nc.vector.tensor_tensor(
                    out=by_tile_and_i(scale[:, lo : lo + count, :]),
                    in0=by_tile_and_i(sums[:, lo : lo + count, :]),
                    in1=repeat_i(offset, n, count), op=ALU.add,
                )
            nc.sync.dma_start(out=scale_rows[:, tiles_of(s), :], in_=scale[:])

        def logs(s):
            if s == 0:
                variance(s)
            summands(s)
            sum_over_g(s)
            if s + 1 < UNITS:
                variance(s + 1)
            log_scale(s)

        nc.scalar.activation(
            out=as_njtg(half_inv_a), in_=repeat_t(svar), func=ACT.Exp, scale=-2.0
        )
        quantise_weights()
        for s in range(-AHEAD_TRANSPOSE, AHEAD_FRONT):
            front(s)
            if s == -AHEAD_QUANTISE:
                spread_state()
        jobs = [(products, s) for s in range(UNITS)] + [(logs, s) for s in range(UNITS)]
        for index, (job, s) in enumerate(jobs):
            ahead = index + AHEAD_LN - UNITS
            if 0 <= ahead < UNITS:
                log_weight(ahead)
            if 0 <= ahead - 1 < UNITS:
                half_log(ahead - 1)
            job(s)
            if index + AHEAD_FRONT < UNITS:
                front(index + AHEAD_FRONT)
